import numpy as np
import ml_dtypes

BF16 = ml_dtypes.bfloat16


def bf(x):
    return np.asarray(x, np.float32).astype(BF16)


def f32(x):
    return np.asarray(x, np.float32)


def f64(x):
    return np.asarray(x).astype(np.float64)


def striped(idx):
    return np.tile(idx.reshape(-1, 16).T, (8, 1))


C, S, N, B, T, H, DH = 512, 4096, 2048, 4, 512, 4, 128
EPS = 1e-5
PE_BASE = 10000.0


def pos_encoding():
    pos = np.arange(T, dtype=np.float64)[None, :]
    ch = np.arange(C)[:, None]
    even = (ch - ch % 2).astype(np.float64)
    ang = pos * PE_BASE ** (-even / C)
    return np.where(ch % 2 == 0, np.sin(ang), np.cos(ang))


def heads(m):
    return m.reshape(H, DH, B, T).transpose(2, 0, 1, 3)


def setup_inputs():
    rn = np.random.standard_normal
    return {"emb": f32(rn((C, S))), "pe": f32(pos_encoding()), "wq": bf(rn((C, C)) / np.sqrt(C)), "bq": f32(0.2 * rn((C, 1))), "wk": bf(rn((C, C)) / np.sqrt(C)), "wv": bf(rn((C, C)) / np.sqrt(C)), "bv": f32(0.1 * rn((C, 1))), "wo": bf(rn((C, C)) / np.sqrt(C)), "bo": f32(0.1 * rn((C, 1))), "ln_w": f32(1.0 + 0.1 * rn((C, 1))), "ln_b": f32(0.1 * rn((C, 1))), "offs": striped(np.random.permutation(np.tile(np.arange(S), 2))[:N])}


def reference(emb, pe, wq, bq, wk, wv, bv, wo, bo, ln_w, ln_b, offs):
    idx = offs[:16].T.reshape(-1)
    x = f64(emb)[:, idx] + np.tile(f64(pe), (1, B))
    q = f64(wq).T @ x + f64(bq)
    k = f64(wk).T @ x
    v = f64(wv).T @ x + f64(bv)
    qh, kh, vh = heads(q), heads(k), heads(v)
    a = qh.transpose(0, 1, 3, 2) @ kh / np.sqrt(DH)
    a = np.where(np.tril(np.ones((T, T), bool)), a, -np.inf)
    p = np.exp(a - a.max(-1, keepdims=True))
    p = p / p.sum(-1, keepdims=True)
    y = vh @ p.transpose(0, 1, 3, 2)
    y = y.transpose(1, 2, 0, 3).reshape(C, N)
    z = x + f64(wo).T @ y + f64(bo)
    mu = z.mean(0, keepdims=True)
    var = ((z - mu) ** 2).mean(0, keepdims=True)
    return (z - mu) / np.sqrt(var + EPS) * f64(ln_w) + f64(ln_b)

@@ -1,0 +1,213 @@
+import math
+from contextlib import ExitStack
+
+import concourse.mybir as mybir
+from concourse.masks import make_identity
+
+F32 = mybir.dt.float32
+BF16 = mybir.dt.bfloat16
+U16 = mybir.dt.uint16
+ALU = mybir.AluOpType
+FUNC = mybir.ActivationFunctionType
+
+P = 128
+C, S, N, B, T, H = 512, 4096, 2048, 4, 512, 4
+CB = C // P
+TB = T // P
+EPS = 1e-5
+INV_SQRT_DH = 1.0 / math.sqrt(P)
+MASKED = -1e30
+ROWS = 64
+BQ, BO, LN_W, LN_B = 0, 1, 2, 3
+
+FLOPS = 4 * 2 * C * C * N + 2 * 2 * P * (T * (T + 1) // 2) * B * H
+
+
+def tile_captioningtransformer_b_kernel(tc, emb, pe, wq, bq, wk, wv, bv, wo, bo, ln_w, ln_b, offs, out):
+    nc = tc.nc
+    with ExitStack() as ctx:
+        held = ctx.enter_context(tc.tile_pool(name="held", bufs=1))
+        caption = ctx.enter_context(tc.tile_pool(name="caption", bufs=2))
+        block = ctx.enter_context(tc.tile_pool(name="block", bufs=3))
+        norm = ctx.enter_context(tc.tile_pool(name="norm", bufs=1))
+        acc = ctx.enter_context(tc.psum_pool(name="acc", bufs=2))
+        score = ctx.enter_context(tc.psum_pool(name="score", bufs=2))
+        flip = ctx.enter_context(tc.psum_pool(name="flip", bufs=2))
+        mixed = ctx.enter_context(tc.psum_pool(name="mixed", bufs=2))
+
+        offsets = held.tile([P, N // 16], U16, name="offsets")
+        nc.sync.dma_start(offsets[:], offs)
+        table = [held.tile([P, S], F32, name=f"table{cb}") for cb in range(CB)]
+        for cb in range(CB):
+            nc.sync.dma_start(table[cb][:], emb[cb * P : (cb + 1) * P, :])
+        pos = held.tile([P, CB, T], F32, name="pos")
+        nc.scalar.dma_start(pos[:], pe.rearrange("(cb p) t -> p cb t", p=P))
+        wq_sb = held.tile([P, CB, C], BF16, name="wq_sb")
+        nc.scalar.dma_start(wq_sb[:], wq.rearrange("(cb p) m -> p cb m", p=P))
+        wk_sb = held.tile([P, CB, C], BF16, name="wk_sb")
+        nc.sync.dma_start(wk_sb[:], wk.rearrange("(cb p) m -> p cb m", p=P))
+        wv_sb = held.tile([P, CB, C], BF16, name="wv_sb")
+        nc.sync.dma_start(wv_sb[:], wv.rearrange("(cb p) m -> p cb m", p=P))
+        wo_sb = held.tile([P, CB, C], BF16, name="wo_sb")
+        nc.sync.dma_start(wo_sb[:], wo.rearrange("(cb p) m -> p cb m", p=P))
+
+        bv_rows = held.tile([P, C], F32, name="bv_rows")
+        nc.gpsimd.dma_start(bv_rows[:], bv.rearrange("c one -> (c one)").partition_broadcast(P))
+
+        rows = held.tile([ROWS, C], F32, name="rows")
+        nc.vector.memset(rows[:], 0.0)
+        for r, vector in ((BQ, bq), (BO, bo), (LN_W, ln_w), (LN_B, ln_b)):
+            nc.gpsimd.dma_start(rows[r : r + 1, :], vector.rearrange("c one -> one c"))
+        ident_f32 = held.tile([ROWS, ROWS], F32, name="ident_f32")
+        make_identity(nc, ident_f32[:])
+        vectors_ps = acc.tile([P, T], F32, name="vectors_ps", tag="acc")
+        for cb in range(CB):
+            nc.tensor.transpose(vectors_ps[:, cb * ROWS : (cb + 1) * ROWS], rows[:, cb * P : (cb + 1) * P], ident_f32[:])
+        vectors = held.tile([P, CB, 4], F32, name="vectors")
+        nc.vector.tensor_copy(vectors[:], vectors_ps[:, : CB * ROWS].rearrange("p (cb r) -> p cb r", r=ROWS)[:, :, 0:4])
+        bq_scaled = held.tile([P, CB], F32, name="bq_scaled")
+        nc.vector.tensor_scalar_mul(bq_scaled[:], vectors[:, :, BQ], INV_SQRT_DH)
+
+        ident = held.tile([P, P], BF16, name="ident")
+        make_identity(nc, ident[:])
+        mask_f32 = held.tile([P, P], F32, name="mask_f32")
+        nc.gpsimd.memset(mask_f32[:], 0.0)
+        nc.gpsimd.affine_select(
+            out=mask_f32[:],
+            in_=mask_f32[:],
+            compare_op=ALU.is_ge,
+            fill=MASKED,
+            base=0,
+            pattern=[[-1, P]],
+            channel_multiplier=1,
+        )
+        mask = held.tile([P, P], BF16, name="mask")
+        nc.vector.tensor_copy(mask[:], mask_f32[:])
+        averager = held.tile([P, P], BF16, name="averager")
+        nc.vector.memset(averager[:], 1.0 / C)
+        eps = held.tile([P, 1], F32, name="eps")
+        nc.vector.memset(eps[:], EPS)
+
+        x = [held.tile([P, N], F32, name=f"x{cb}") for cb in range(CB)]
+        x_bf = [held.tile([P, N], BF16, name=f"x_bf{cb}") for cb in range(CB)]
+        for cb in range(CB):
+            for b in range(B):
+                entries = slice(b * T, (b + 1) * T)
+                picked = table[cb][:].indirect(offsets[:, b * T // 16 : (b + 1) * T // 16])
+                nc.vector.tensor_tensor(x[cb][:, entries], picked, pos[:, cb, :], ALU.add)
+                nc.gpsimd.tensor_copy(x_bf[cb][:, entries], x[cb][:, entries])
+
+        q_bf, k_bf, vT_bf, y_bf = {}, {}, {}, {}
+
+        def project(b):
+            entries = slice(b * T, (b + 1) * T)
+            q_bf[b] = caption.tile([P, H, T], BF16, name="q_bf")
+            k_bf[b] = caption.tile([P, H, T], BF16, name="k_bf")
+            vT_bf[b] = caption.tile([P, TB, C], BF16, name="vT_bf")
+            for h in range(H):
+                head = slice(h * P, (h + 1) * P)
+                q_ps = acc.tile([P, T], F32, name="q_ps", tag="acc")
+                for cb in range(CB):
+                    nc.tensor.matmul(q_ps[:], wq_sb[:, cb, head], x_bf[cb][:, entries], start=cb == 0, stop=cb == CB - 1)
+                nc.scalar.activation(
+                    q_bf[b][:, h, :], q_ps[:], FUNC.Identity, bias=bq_scaled[:, h : h + 1], scale=INV_SQRT_DH
+                )
+            for h in range(H):
+                head = slice(h * P, (h + 1) * P)
+                k_ps = acc.tile([P, T], F32, name="k_ps", tag="acc")
+                for cb in range(CB):
+                    nc.tensor.matmul(k_ps[:], wk_sb[:, cb, head], x_bf[cb][:, entries], start=cb == 0, stop=cb == CB - 1)
+                nc.scalar.copy(k_bf[b][:, h, :], k_ps[:])
+            for ib in range(TB):
+                keys = slice(b * T + ib * P, b * T + (ib + 1) * P)
+                v_ps = acc.tile([P, C], F32, name="v_ps", tag="acc")
+                for cb in range(CB):
+                    nc.tensor.matmul(v_ps[:], x_bf[cb][:, keys], wv_sb[:, cb, :], start=cb == 0, stop=cb == CB - 1)
+                nc.vector.tensor_tensor(vT_bf[b][:, ib, :], v_ps[:], bv_rows[:], ALU.add)
+
+        def attend(b, h):
+            head = slice(h * P, (h + 1) * P)
+            y_ps = mixed.tile([P, T], F32, name="y_ps")
+            for jb in range(TB):
+                width = (jb + 1) * P
+                queries = slice(jb * P, width)
+                s_ps = score.tile([P, T], F32, name="s_ps")
+                nc.tensor.matmul(s_ps[:, :width], q_bf[b][:, h, queries], k_bf[b][:, h, :width], start=True, stop=False)
+                nc.tensor.matmul(s_ps[:, queries], ident[:], mask[:], start=False, stop=True)
+
+                minus_max = block.tile([P, 1], F32, name="minus_max")
+                nc.vector.reduce_max(minus_max[:], s_ps[:, :width], axis=mybir.AxisListType.X, negate=True)
+                e = block.tile([P, T], F32, name="e")
+                e_sum = block.tile([P, 1], F32, name="e_sum")
+                nc.scalar.activation(e[:, :width], s_ps[:, :width], FUNC.Exp, bias=minus_max[:], accum_out=e_sum[:])
+                inv_sum = block.tile([P, 1], F32, name="inv_sum")
+                nc.vector.reciprocal(inv_sum[:], e_sum[:])
+                p_bf = block.tile([P, T], BF16, name="p_bf")
+                nc.gpsimd.tensor_scalar(p_bf[:, :width], e[:, :width], inv_sum[:], 1.0, ALU.mult, ALU.mult)
+
+                pT_ps = flip.tile([P, T], BF16, name="pT_ps")
+                for ib in range(jb + 1):
+                    keys = slice(ib * P, (ib + 1) * P)
+                    nc.tensor.transpose(pT_ps[:, keys], p_bf[:, keys], ident[:])
+                pT_bf = block.tile([P, T], BF16, name="pT_bf")
+                nc.vector.tensor_copy(pT_bf[:, :width], pT_ps[:, :width])
+                for ib in range(jb + 1):
+                    keys = slice(ib * P, (ib + 1) * P)
+                    nc.tensor.matmul(y_ps[:, queries], vT_bf[b][:, ib, head], pT_bf[:, keys], start=ib == 0, stop=ib == jb)
+            nc.scalar.copy(y_bf[b][:, h, :], y_ps[:])
+
+        def finish(b):
+            entries = slice(b * T, (b + 1) * T)
+            z = norm.tile([P, CB, T], F32, name="z")
+            z_bf = norm.tile([P, CB, T], BF16, name="z_bf")
+            for mb in range(CB):
+                z_ps = acc.tile([P, T], F32, name="z_ps", tag="acc")
+                for cb in range(CB):
+                    nc.tensor.matmul(
+                        z_ps[:], wo_sb[:, cb, mb * P : (mb + 1) * P], y_bf[b][:, cb, :], start=cb == 0, stop=cb == CB - 1
+                    )
+                nc.vector.scalar_tensor_tensor(
+                    z[:, mb, :], z_ps[:], vectors[:, mb, BO : BO + 1], x[mb][:, entries], ALU.add, ALU.add
+                )
+                nc.gpsimd.tensor_copy(z_bf[:, mb, :], z[:, mb, :])
+
+            mean_ps = acc.tile([P, T], F32, name="mean_ps", tag="acc")
+            for mb in range(CB):
+                nc.tensor.matmul(mean_ps[:], averager[:], z_bf[:, mb, :], start=mb == 0, stop=mb == CB - 1)
+            centred = norm.tile([P, CB, T], F32, name="centred")
+            squares = norm.tile([P, CB, T], BF16, name="squares")
+            for mb in range(CB):
+                nc.vector.tensor_tensor(centred[:, mb, :], z[:, mb, :], mean_ps[:], ALU.subtract)
+                nc.scalar.square(squares[:, mb, :], centred[:, mb, :])
+            var_ps = acc.tile([P, T], F32, name="var_ps", tag="acc")
+            for mb in range(CB):
+                nc.tensor.matmul(var_ps[:], averager[:], squares[:, mb, :], start=mb == 0, stop=mb == CB - 1)
+
+            log_var = norm.tile([P, T], F32, name="log_var")
+            nc.scalar.activation(log_var[:], var_ps[:], FUNC.Ln, bias=eps[:])
+            inv_std = norm.tile([P, T], F32, name="inv_std")
+            nc.scalar.activation(inv_std[:], log_var[:], FUNC.Exp, scale=-0.5)
+
+            normed = norm.tile([P, CB, T], F32, name="normed")
+            result = norm.tile([P, CB, T], F32, name="result")
+            for mb in range(CB):
+                nc.vector.tensor_tensor(normed[:, mb, :], centred[:, mb, :], inv_std[:], ALU.mult)
+                nc.scalar.activation(
+                    result[:, mb, :],
+                    normed[:, mb, :],
+                    FUNC.Identity,
+                    bias=vectors[:, mb, LN_B : LN_B + 1],
+                    scale=vectors[:, mb, LN_W : LN_W + 1],
+                )
+                nc.sync.dma_start(out[mb * P : (mb + 1) * P, entries], result[:, mb, :])
+
+        project(0)
+        for b in range(B):
+            y_bf[b] = caption.tile([P, H, T], BF16, name="y_bf")
+            for h in range(H):
+                attend(b, h)
+            if b + 1 < B:
+                project(b + 1)
+            if b >= 1:
+                finish(b - 1)
+        finish(B - 1)

@@ -27,97 +27,126 @@ def tile_captioningtransformer_b_kernel(tc, emb, pe, wq, bq, wk, wv, bv, wo, bo,
     nc = tc.nc
     with ExitStack() as ctx:
         held = ctx.enter_context(tc.tile_pool(name="held", bufs=1))
-        caption = ctx.enter_context(tc.tile_pool(name="caption", bufs=2))
-        block = ctx.enter_context(tc.tile_pool(name="block", bufs=3))
-        norm = ctx.enter_context(tc.tile_pool(name="norm", bufs=1))
-        acc = ctx.enter_context(tc.psum_pool(name="acc", bufs=2))
-        score = ctx.enter_context(tc.psum_pool(name="score", bufs=2))
-        flip = ctx.enter_context(tc.psum_pool(name="flip", bufs=2))
-        mixed = ctx.enter_context(tc.psum_pool(name="mixed", bufs=2))
+        caption = ctx.enter_context(tc.tile_pool(name="caption", bufs=3))
 
         offsets = held.tile([P, N // 16], U16, name="offsets")
         nc.sync.dma_start(offsets[:], offs)
-        table = [held.tile([P, S], F32, name=f"table{cb}") for cb in range(CB)]
-        for cb in range(CB):
-            nc.sync.dma_start(table[cb][:], emb[cb * P : (cb + 1) * P, :])
-        pos = held.tile([P, CB, T], F32, name="pos")
-        nc.scalar.dma_start(pos[:], pe.rearrange("(cb p) t -> p cb t", p=P))
-        wq_sb = held.tile([P, CB, C], BF16, name="wq_sb")
-        nc.scalar.dma_start(wq_sb[:], wq.rearrange("(cb p) m -> p cb m", p=P))
-        wk_sb = held.tile([P, CB, C], BF16, name="wk_sb")
-        nc.sync.dma_start(wk_sb[:], wk.rearrange("(cb p) m -> p cb m", p=P))
-        wv_sb = held.tile([P, CB, C], BF16, name="wv_sb")
-        nc.sync.dma_start(wv_sb[:], wv.rearrange("(cb p) m -> p cb m", p=P))
-        wo_sb = held.tile([P, CB, C], BF16, name="wo_sb")
-        nc.sync.dma_start(wo_sb[:], wo.rearrange("(cb p) m -> p cb m", p=P))
-
-        bv_rows = held.tile([P, C], F32, name="bv_rows")
-        nc.gpsimd.dma_start(bv_rows[:], bv.rearrange("c one -> (c one)").partition_broadcast(P))
-
-        rows = held.tile([ROWS, C], F32, name="rows")
-        nc.vector.memset(rows[:], 0.0)
-        for r, vector in ((BQ, bq), (BO, bo), (LN_W, ln_w), (LN_B, ln_b)):
-            nc.gpsimd.dma_start(rows[r : r + 1, :], vector.rearrange("c one -> one c"))
-        ident_f32 = held.tile([ROWS, ROWS], F32, name="ident_f32")
-        make_identity(nc, ident_f32[:])
-        vectors_ps = acc.tile([P, T], F32, name="vectors_ps", tag="acc")
-        for cb in range(CB):
-            nc.tensor.transpose(vectors_ps[:, cb * ROWS : (cb + 1) * ROWS], rows[:, cb * P : (cb + 1) * P], ident_f32[:])
-        vectors = held.tile([P, CB, 4], F32, name="vectors")
-        nc.vector.tensor_copy(vectors[:], vectors_ps[:, : CB * ROWS].rearrange("p (cb r) -> p cb r", r=ROWS)[:, :, 0:4])
-        bq_scaled = held.tile([P, CB], F32, name="bq_scaled")
-        nc.vector.tensor_scalar_mul(bq_scaled[:], vectors[:, :, BQ], INV_SQRT_DH)
-
-        ident = held.tile([P, P], BF16, name="ident")
-        make_identity(nc, ident[:])
-        mask_f32 = held.tile([P, P], F32, name="mask_f32")
-        nc.gpsimd.memset(mask_f32[:], 0.0)
-        nc.gpsimd.affine_select(
-            out=mask_f32[:],
-            in_=mask_f32[:],
-            compare_op=ALU.is_ge,
-            fill=MASKED,
-            base=0,
-            pattern=[[-1, P]],
-            channel_multiplier=1,
-        )
-        mask = held.tile([P, P], BF16, name="mask")
-        nc.vector.tensor_copy(mask[:], mask_f32[:])
-        averager = held.tile([P, P], BF16, name="averager")
-        nc.vector.memset(averager[:], 1.0 / C)
-        eps = held.tile([P, 1], F32, name="eps")
-        nc.vector.memset(eps[:], EPS)
 
         x = [held.tile([P, N], F32, name=f"x{cb}") for cb in range(CB)]
         x_bf = [held.tile([P, N], BF16, name=f"x_bf{cb}") for cb in range(CB)]
-        for cb in range(CB):
-            for b in range(B):
-                entries = slice(b * T, (b + 1) * T)
-                picked = table[cb][:].indirect(offsets[:, b * T // 16 : (b + 1) * T // 16])
-                nc.vector.tensor_tensor(x[cb][:, entries], picked, pos[:, cb, :], ALU.add)
-                nc.gpsimd.tensor_copy(x_bf[cb][:, entries], x[cb][:, entries])
-
         q_bf, k_bf, vT_bf, y_bf = {}, {}, {}, {}
 
-        def project(b):
-            entries = slice(b * T, (b + 1) * T)
+        def new_caption(b):
             q_bf[b] = caption.tile([P, H, T], BF16, name="q_bf")
             k_bf[b] = caption.tile([P, H, T], BF16, name="k_bf")
             vT_bf[b] = caption.tile([P, TB, C], BF16, name="vT_bf")
+            y_bf[b] = caption.tile([P, H, T], BF16, name="y_bf")
+
+        def store_q(b, h, q_ps):
+            nc.scalar.activation(q_bf[b][:, h, :], q_ps[:], FUNC.Identity, bias=bq_scaled[:, h : h + 1], scale=INV_SQRT_DH)
+
+        def store_k(b, h, k_ps):
+            nc.scalar.copy(k_bf[b][:, h, :], k_ps[:])
+
+        with tc.tile_pool(name="start", bufs=1) as start:
+            rows = start.tile([ROWS, C], F32, name="rows")
+            nc.vector.memset(rows[:], 0.0)
+            for r, vector in ((BQ, bq), (BO, bo), (LN_W, ln_w), (LN_B, ln_b)):
+                nc.sync.dma_start(rows[r : r + 1, :], vector.rearrange("c one -> one c"))
+            pos = start.tile([P, CB, T], F32, name="pos")
+            nc.sync.dma_start(pos[:], pe.rearrange("(cb p) t -> p cb t", p=P))
+            table = [start.tile([P, S], F32, name=f"table{cb}") for cb in range(CB)]
+            nc.sync.dma_start(table[0][:], emb[0:P, :])
+            wq_sb = held.tile([P, CB, C], BF16, name="wq_sb")
+            nc.sync.dma_start(wq_sb[:], wq.rearrange("(cb p) m -> p cb m", p=P))
+            wk_sb = held.tile([P, CB, C], BF16, name="wk_sb")
+            nc.sync.dma_start(wk_sb[:], wk.rearrange("(cb p) m -> p cb m", p=P))
+            for cb in range(1, CB):
+                nc.sync.dma_start(table[cb][:], emb[cb * P : (cb + 1) * P, :])
+            wv_sb = held.tile([P, CB, C], BF16, name="wv_sb")
+            nc.sync.dma_start(wv_sb[:], wv.rearrange("(cb p) m -> p cb m", p=P))
+            bv_rows = held.tile([P, C], F32, name="bv_rows")
+            nc.sync.dma_start(bv_rows[:], bv.rearrange("c one -> (c one)").partition_broadcast(P))
+            wo_sb = held.tile([P, CB, C], BF16, name="wo_sb")
+            nc.sync.dma_start(wo_sb[:], wo.rearrange("(cb p) m -> p cb m", p=P))
+
+            ident_f32 = start.tile([ROWS, ROWS], F32, name="ident_f32")
+            make_identity(nc, ident_f32[:])
+            vectors = held.tile([P, CB, 4], F32, name="vectors")
+            with tc.psum_pool(name="turned", bufs=1) as turned:
+                vectors_ps = turned.tile([P, CB, ROWS], F32, name="vectors_ps")
+                for cb in range(CB):
+                    nc.tensor.transpose(vectors_ps[:, cb, :], rows[:, cb * P : (cb + 1) * P], ident_f32[:])
+                nc.vector.tensor_copy(vectors[:], vectors_ps[:, :, 0:4])
+            bq_scaled = held.tile([P, CB], F32, name="bq_scaled")
+            nc.vector.tensor_scalar_mul(bq_scaled[:], vectors[:, :, BQ], INV_SQRT_DH)
+
+            ident = held.tile([P, P], BF16, name="ident")
+            make_identity(nc, ident[:])
+            mask_f32 = start.tile([P, P], F32, name="mask_f32")
+            nc.gpsimd.memset(mask_f32[:], 0.0)
+            nc.gpsimd.affine_select(
+                out=mask_f32[:],
+                in_=mask_f32[:],
+                compare_op=ALU.is_ge,
+                fill=MASKED,
+                base=0,
+                pattern=[[-1, P]],
+                channel_multiplier=1,
+            )
+            mask = held.tile([P, P], BF16, name="mask")
+            nc.vector.tensor_copy(mask[:], mask_f32[:])
+            averager = held.tile([P, P], BF16, name="averager")
+            nc.vector.memset(averager[:], 1.0 / C)
+            eps = held.tile([P, 1], F32, name="eps")
+            nc.vector.memset(eps[:], EPS)
+
+            def look_up(cb, b):
+                entries = slice(b * T, (b + 1) * T)
+                picked = table[cb][:].indirect(offsets[:, b * T // 16 : (b + 1) * T // 16])
+                nc.vector.tensor_tensor(x[cb][:, entries], picked, pos[:, cb, :], ALU.add)
+                nc.scalar.copy(x_bf[cb][:, entries], x[cb][:, entries])
+
+            new_caption(0)
+            with tc.psum_pool(name="first", bufs=1) as first:
+                q_ps = [first.tile([P, T], F32, name=f"q_ps{h}") for h in range(H)]
+                k_ps = [first.tile([P, T], F32, name=f"k_ps{h}") for h in range(H)]
+                for cb in range(CB):
+                    look_up(cb, 0)
+                    for h in range(H):
+                        head = slice(h * P, (h + 1) * P)
+                        nc.tensor.matmul(q_ps[h][:], wq_sb[:, cb, head], x_bf[cb][:, :T], start=cb == 0, stop=cb == CB - 1)
+                        nc.tensor.matmul(k_ps[h][:], wk_sb[:, cb, head], x_bf[cb][:, :T], start=cb == 0, stop=cb == CB - 1)
+                for h in range(H):
+                    store_q(0, h, q_ps[h])
+                    store_k(0, h, k_ps[h])
+            for cb in range(CB):
+                for b in range(1, B):
+                    look_up(cb, b)
+
+        block = ctx.enter_context(tc.tile_pool(name="block", bufs=4))
+        flipped = ctx.enter_context(tc.tile_pool(name="flipped", bufs=2))
+        norm = ctx.enter_context(tc.tile_pool(name="norm", bufs=2))
+        acc = ctx.enter_context(tc.psum_pool(name="acc", bufs=2))
+        stat = ctx.enter_context(tc.psum_pool(name="stat", bufs=1))
+        score = ctx.enter_context(tc.psum_pool(name="score", bufs=2))
+        flip = ctx.enter_context(tc.psum_pool(name="flip", bufs=2))
+        mixed = ctx.enter_context(tc.psum_pool(name="mixed", bufs=1))
+
+        def project_qk(b):
+            entries = slice(b * T, (b + 1) * T)
             for h in range(H):
                 head = slice(h * P, (h + 1) * P)
                 q_ps = acc.tile([P, T], F32, name="q_ps", tag="acc")
                 for cb in range(CB):
                     nc.tensor.matmul(q_ps[:], wq_sb[:, cb, head], x_bf[cb][:, entries], start=cb == 0, stop=cb == CB - 1)
-                nc.scalar.activation(
-                    q_bf[b][:, h, :], q_ps[:], FUNC.Identity, bias=bq_scaled[:, h : h + 1], scale=INV_SQRT_DH
-                )
-            for h in range(H):
-                head = slice(h * P, (h + 1) * P)
+                store_q(b, h, q_ps)
                 k_ps = acc.tile([P, T], F32, name="k_ps", tag="acc")
                 for cb in range(CB):
                     nc.tensor.matmul(k_ps[:], wk_sb[:, cb, head], x_bf[cb][:, entries], start=cb == 0, stop=cb == CB - 1)
-                nc.scalar.copy(k_bf[b][:, h, :], k_ps[:])
+                store_k(b, h, k_ps)
+
+        def project_v(b):
             for ib in range(TB):
                 keys = slice(b * T + ib * P, b * T + (ib + 1) * P)
                 v_ps = acc.tile([P, C], F32, name="v_ps", tag="acc")
@@ -127,7 +156,7 @@ def tile_captioningtransformer_b_kernel(tc, emb, pe, wq, bq, wk, wv, bv, wo, bo,
 
         def attend(b, h):
             head = slice(h * P, (h + 1) * P)
-            y_ps = mixed.tile([P, T], F32, name="y_ps")
+            pT_bf = flipped.tile([P, TB, T], BF16, name="pT_bf")
             for jb in range(TB):
                 width = (jb + 1) * P
                 queries = slice(jb * P, width)
@@ -143,23 +172,32 @@ def tile_captioningtransformer_b_kernel(tc, emb, pe, wq, bq, wk, wv, bv, wo, bo,
                 inv_sum = block.tile([P, 1], F32, name="inv_sum")
                 nc.vector.reciprocal(inv_sum[:], e_sum[:])
                 p_bf = block.tile([P, T], BF16, name="p_bf")
-                nc.gpsimd.tensor_scalar(p_bf[:, :width], e[:, :width], inv_sum[:], 1.0, ALU.mult, ALU.mult)
+                nc.vector.tensor_scalar_mul(p_bf[:, :width], e[:, :width], inv_sum[:])
 
-                pT_ps = flip.tile([P, T], BF16, name="pT_ps")
+                pT_ps = flip.tile([P, TB, P], BF16, name="pT_ps")
                 for ib in range(jb + 1):
-                    keys = slice(ib * P, (ib + 1) * P)
-                    nc.tensor.transpose(pT_ps[:, keys], p_bf[:, keys], ident[:])
-                pT_bf = block.tile([P, T], BF16, name="pT_bf")
-                nc.vector.tensor_copy(pT_bf[:, :width], pT_ps[:, :width])
-                for ib in range(jb + 1):
-                    keys = slice(ib * P, (ib + 1) * P)
-                    nc.tensor.matmul(y_ps[:, queries], vT_bf[b][:, ib, head], pT_bf[:, keys], start=ib == 0, stop=ib == jb)
+                    nc.tensor.transpose(pT_ps[:, ib, :], p_bf[:, ib * P : (ib + 1) * P], ident[:])
+                nc.vector.tensor_copy(pT_bf[:, : jb + 1, queries], pT_ps[:, : jb + 1, :])
+            y_ps = mixed.tile([P, T], F32, name="y_ps")
+            for ib in range(TB):
+                nc.tensor.matmul(
+                    y_ps[:, ib * P :], vT_bf[b][:, ib, head], pT_bf[:, ib, ib * P :], start=ib == 0, stop=ib == TB - 1
+                )
             nc.scalar.copy(y_bf[b][:, h, :], y_ps[:])
+
+        def mean_over_features(blocks, name):
+            partial = norm.tile([P, T], F32, name="partial")
+            nc.gpsimd.tensor_tensor(partial[:], blocks[:, 0, :], blocks[:, 1, :], ALU.add)
+            nc.gpsimd.tensor_tensor(partial[:], partial[:], blocks[:, 2, :], ALU.add)
+            partial_bf = norm.tile([P, T], BF16, name="partial_bf")
+            nc.vector.tensor_tensor(partial_bf[:], partial[:], blocks[:, 3, :], ALU.add)
+            mean_ps = stat.tile([P, T], F32, name=name, tag="stat")
+            nc.tensor.matmul(mean_ps[:], averager[:], partial_bf[:], start=True, stop=True)
+            return mean_ps
 
         def finish(b):
             entries = slice(b * T, (b + 1) * T)
             z = norm.tile([P, CB, T], F32, name="z")
-            z_bf = norm.tile([P, CB, T], BF16, name="z_bf")
             for mb in range(CB):
                 z_ps = acc.tile([P, T], F32, name="z_ps", tag="acc")
                 for cb in range(CB):
@@ -169,19 +207,14 @@ def tile_captioningtransformer_b_kernel(tc, emb, pe, wq, bq, wk, wv, bv, wo, bo,
                 nc.vector.scalar_tensor_tensor(
                     z[:, mb, :], z_ps[:], vectors[:, mb, BO : BO + 1], x[mb][:, entries], ALU.add, ALU.add
                 )
-                nc.gpsimd.tensor_copy(z_bf[:, mb, :], z[:, mb, :])
 
-            mean_ps = acc.tile([P, T], F32, name="mean_ps", tag="acc")
-            for mb in range(CB):
-                nc.tensor.matmul(mean_ps[:], averager[:], z_bf[:, mb, :], start=mb == 0, stop=mb == CB - 1)
+            mean_ps = mean_over_features(z, "mean_ps")
             centred = norm.tile([P, CB, T], F32, name="centred")
-            squares = norm.tile([P, CB, T], BF16, name="squares")
+            squares = norm.tile([P, CB, T], F32, name="squares")
             for mb in range(CB):
                 nc.vector.tensor_tensor(centred[:, mb, :], z[:, mb, :], mean_ps[:], ALU.subtract)
                 nc.scalar.square(squares[:, mb, :], centred[:, mb, :])
-            var_ps = acc.tile([P, T], F32, name="var_ps", tag="acc")
-            for mb in range(CB):
-                nc.tensor.matmul(var_ps[:], averager[:], squares[:, mb, :], start=mb == 0, stop=mb == CB - 1)
+            var_ps = mean_over_features(squares, "var_ps")
 
             log_var = norm.tile([P, T], F32, name="log_var")
             nc.scalar.activation(log_var[:], var_ps[:], FUNC.Ln, bias=eps[:])
@@ -201,13 +234,14 @@ def tile_captioningtransformer_b_kernel(tc, emb, pe, wq, bq, wk, wv, bv, wo, bo,
                 )
                 nc.sync.dma_start(out[mb * P : (mb + 1) * P, entries], result[:, mb, :])
 
-        project(0)
+        project_v(0)
         for b in range(B):
-            y_bf[b] = caption.tile([P, H, T], BF16, name="y_bf")
             for h in range(H):
                 attend(b, h)
             if b + 1 < B:
-                project(b + 1)
+                new_caption(b + 1)
+                project_qk(b + 1)
+                project_v(b + 1)
             if b >= 1:
                 finish(b - 1)
         finish(B - 1)

@@ -18,7 +18,7 @@ EPS = 1e-5
 INV_SQRT_DH = 1.0 / math.sqrt(P)
 MASKED = -1e30
 ROWS = 64
-BQ, BO, LN_W, LN_B = 0, 1, 2, 3
+BO, BQ, LN_W, LN_B = 0, 1, 2, 3
 
 FLOPS = 4 * 2 * C * C * N + 2 * 2 * P * (T * (T + 1) // 2) * B * H
 
@@ -51,7 +51,7 @@ def tile_captioningtransformer_b_kernel(tc, emb, pe, wq, bq, wk, wv, bv, wo, bo,
         with tc.tile_pool(name="start", bufs=1) as start:
             rows = start.tile([ROWS, C], F32, name="rows")
             nc.vector.memset(rows[:], 0.0)
-            for r, vector in ((BQ, bq), (BO, bo), (LN_W, ln_w), (LN_B, ln_b)):
+            for r, vector in ((BO, bo), (BQ, bq), (LN_W, ln_w), (LN_B, ln_b)):
                 nc.sync.dma_start(rows[r : r + 1, :], vector.rearrange("c one -> one c"))
             pos = start.tile([P, CB, T], F32, name="pos")
             nc.sync.dma_start(pos[:], pe.rearrange("(cb p) t -> p cb t", p=P))
@@ -69,6 +69,11 @@ def tile_captioningtransformer_b_kernel(tc, emb, pe, wq, bq, wk, wv, bv, wo, bo,
             nc.sync.dma_start(bv_rows[:], bv.rearrange("c one -> (c one)").partition_broadcast(P))
             wo_sb = held.tile([P, CB, C], BF16, name="wo_sb")
             nc.sync.dma_start(wo_sb[:], wo.rearrange("(cb p) m -> p cb m", p=P))
+
+            bo_shift = start.tile([1, 1], F32, name="bo_shift")
+            nc.vector.reduce_sum(bo_shift[:], rows[BO : BO + 1, :], axis=mybir.AxisListType.X)
+            nc.vector.tensor_scalar_mul(bo_shift[:], bo_shift[:], -1.0 / C)
+            nc.vector.tensor_scalar_add(rows[BO : BO + 1, :], rows[BO : BO + 1, :], bo_shift[:])
 
             ident_f32 = start.tile([ROWS, ROWS], F32, name="ident_f32")
             make_identity(nc, ident_f32[:])
@@ -127,11 +132,10 @@ def tile_captioningtransformer_b_kernel(tc, emb, pe, wq, bq, wk, wv, bv, wo, bo,
         block = ctx.enter_context(tc.tile_pool(name="block", bufs=4))
         flipped = ctx.enter_context(tc.tile_pool(name="flipped", bufs=2))
         norm = ctx.enter_context(tc.tile_pool(name="norm", bufs=2))
-        acc = ctx.enter_context(tc.psum_pool(name="acc", bufs=2))
-        stat = ctx.enter_context(tc.psum_pool(name="stat", bufs=1))
+        acc = ctx.enter_context(tc.psum_pool(name="acc", bufs=3))
+        rare = ctx.enter_context(tc.psum_pool(name="rare", bufs=1))
         score = ctx.enter_context(tc.psum_pool(name="score", bufs=2))
         flip = ctx.enter_context(tc.psum_pool(name="flip", bufs=2))
-        mixed = ctx.enter_context(tc.psum_pool(name="mixed", bufs=1))
 
         def project_qk(b):
             entries = slice(b * T, (b + 1) * T)
@@ -178,7 +182,7 @@ def tile_captioningtransformer_b_kernel(tc, emb, pe, wq, bq, wk, wv, bv, wo, bo,
                 for ib in range(jb + 1):
                     nc.tensor.transpose(pT_ps[:, ib, :], p_bf[:, ib * P : (ib + 1) * P], ident[:])
                 nc.vector.tensor_copy(pT_bf[:, : jb + 1, queries], pT_ps[:, : jb + 1, :])
-            y_ps = mixed.tile([P, T], F32, name="y_ps")
+            y_ps = rare.tile([P, T], F32, name="y_ps", tag="rare")
             for ib in range(TB):
                 nc.tensor.matmul(
                     y_ps[:, ib * P :], vT_bf[b][:, ib, head], pT_bf[:, ib, ib * P :], start=ib == 0, stop=ib == TB - 1
@@ -187,39 +191,45 @@ def tile_captioningtransformer_b_kernel(tc, emb, pe, wq, bq, wk, wv, bv, wo, bo,
 
         def mean_over_features(blocks, name):
             partial = norm.tile([P, T], F32, name="partial")
-            nc.gpsimd.tensor_tensor(partial[:], blocks[:, 0, :], blocks[:, 1, :], ALU.add)
-            nc.gpsimd.tensor_tensor(partial[:], partial[:], blocks[:, 2, :], ALU.add)
+            nc.gpsimd.tensor_tensor(partial[:], blocks[0], blocks[1], ALU.add)
+            nc.gpsimd.tensor_tensor(partial[:], partial[:], blocks[2], ALU.add)
             partial_bf = norm.tile([P, T], BF16, name="partial_bf")
-            nc.vector.tensor_tensor(partial_bf[:], partial[:], blocks[:, 3, :], ALU.add)
-            mean_ps = stat.tile([P, T], F32, name=name, tag="stat")
+            nc.vector.tensor_tensor(partial_bf[:], partial[:], blocks[3], ALU.add)
+            mean_ps = rare.tile([P, T], F32, name=name, tag="rare")
             nc.tensor.matmul(mean_ps[:], averager[:], partial_bf[:], start=True, stop=True)
             return mean_ps
 
+        wo_shift = held.tile([P, CB], F32, name="wo_shift")
+        nc.vector.reduce_sum(wo_shift[:], wo_sb[:], axis=mybir.AxisListType.X)
+        nc.vector.tensor_scalar_mul(wo_shift[:], wo_shift[:], -1.0 / C)
+        wo_centred = held.tile([P, CB, C], BF16, name="wo_centred")
+        for cb in range(CB):
+            nc.vector.tensor_scalar_add(wo_centred[:, cb, :], wo_sb[:, cb, :], wo_shift[:, cb : cb + 1])
+
+        def centre_x(b):
+            entries = slice(b * T, (b + 1) * T)
+            mean_ps = mean_over_features([x[cb][:, entries] for cb in range(CB)], "mean_ps")
+            for cb in range(CB):
+                nc.vector.tensor_tensor(x[cb][:, entries], x[cb][:, entries], mean_ps[:], ALU.subtract)
+
         def finish(b):
             entries = slice(b * T, (b + 1) * T)
-            z = norm.tile([P, CB, T], F32, name="z")
+            centred = norm.tile([P, CB, T], F32, name="centred")
+            squares = norm.tile([P, CB, T], F32, name="squares")
             for mb in range(CB):
                 z_ps = acc.tile([P, T], F32, name="z_ps", tag="acc")
                 for cb in range(CB):
                     nc.tensor.matmul(
-                        z_ps[:], wo_sb[:, cb, mb * P : (mb + 1) * P], y_bf[b][:, cb, :], start=cb == 0, stop=cb == CB - 1
+                        z_ps[:], wo_centred[:, cb, mb * P : (mb + 1) * P], y_bf[b][:, cb, :], start=cb == 0, stop=cb == CB - 1
                     )
                 nc.vector.scalar_tensor_tensor(
-                    z[:, mb, :], z_ps[:], vectors[:, mb, BO : BO + 1], x[mb][:, entries], ALU.add, ALU.add
+                    centred[:, mb, :], z_ps[:], vectors[:, mb, BO : BO + 1], x[mb][:, entries], ALU.add, ALU.add
                 )
-
-            mean_ps = mean_over_features(z, "mean_ps")
-            centred = norm.tile([P, CB, T], F32, name="centred")
-            squares = norm.tile([P, CB, T], F32, name="squares")
-            for mb in range(CB):
-                nc.vector.tensor_tensor(centred[:, mb, :], z[:, mb, :], mean_ps[:], ALU.subtract)
                 nc.scalar.square(squares[:, mb, :], centred[:, mb, :])
-            var_ps = mean_over_features(squares, "var_ps")
+            var_ps = mean_over_features([squares[:, mb, :] for mb in range(CB)], "var_ps")
 
-            log_var = norm.tile([P, T], F32, name="log_var")
-            nc.scalar.activation(log_var[:], var_ps[:], FUNC.Ln, bias=eps[:])
             inv_std = norm.tile([P, T], F32, name="inv_std")
-            nc.scalar.activation(inv_std[:], log_var[:], FUNC.Exp, scale=-0.5)
+            nc.scalar.activation(inv_std[:], var_ps[:], FUNC.Abs_reciprocal_sqrt, bias=eps[:])
 
             normed = norm.tile([P, CB, T], F32, name="normed")
             result = norm.tile([P, CB, T], F32, name="result")
@@ -235,6 +245,8 @@ def tile_captioningtransformer_b_kernel(tc, emb, pe, wq, bq, wk, wv, bv, wo, bo,
                 nc.sync.dma_start(out[mb * P : (mb + 1) * P, entries], result[:, mb, :])
 
         project_v(0)
+        for b in range(B):
+            centre_x(b)
         for b in range(B):
             for h in range(H):
                 attend(b, h)

@@ -129,8 +129,8 @@ def tile_captioningtransformer_b_kernel(tc, emb, pe, wq, bq, wk, wv, bv, wo, bo,
                 for b in range(1, B):
                     look_up(cb, b)
 
-        block = ctx.enter_context(tc.tile_pool(name="block", bufs=4))
-        flipped = ctx.enter_context(tc.tile_pool(name="flipped", bufs=2))
+        block = ctx.enter_context(tc.tile_pool(name="block", bufs=6))
+        flipped = ctx.enter_context(tc.tile_pool(name="flipped", bufs=3))
         norm = ctx.enter_context(tc.tile_pool(name="norm", bufs=2))
         acc = ctx.enter_context(tc.psum_pool(name="acc", bufs=3))
         rare = ctx.enter_context(tc.psum_pool(name="rare", bufs=1))

@@ -28,6 +28,7 @@ def tile_captioningtransformer_b_kernel(tc, emb, pe, wq, bq, wk, wv, bv, wo, bo,
     with ExitStack() as ctx:
         held = ctx.enter_context(tc.tile_pool(name="held", bufs=1))
         caption = ctx.enter_context(tc.tile_pool(name="caption", bufs=3))
+        softmax = ctx.enter_context(tc.tile_pool(name="softmax", bufs=3))
 
         offsets = held.tile([P, N // 16], U16, name="offsets")
         nc.sync.dma_start(offsets[:], offs)
@@ -43,7 +44,7 @@ def tile_captioningtransformer_b_kernel(tc, emb, pe, wq, bq, wk, wv, bv, wo, bo,
             y_bf[b] = caption.tile([P, H, T], BF16, name="y_bf")
 
         def store_q(b, h, q_ps):
-            nc.scalar.activation(q_bf[b][:, h, :], q_ps[:], FUNC.Identity, bias=bq_scaled[:, h : h + 1], scale=INV_SQRT_DH)
+            nc.scalar.activation(q_bf[b][:, h, :], q_ps[:], FUNC.Identity, bias=vectors[:, h, BQ : BQ + 1])
 
         def store_k(b, h, k_ps):
             nc.scalar.copy(k_bf[b][:, h, :], k_ps[:])
@@ -83,8 +84,6 @@ def tile_captioningtransformer_b_kernel(tc, emb, pe, wq, bq, wk, wv, bv, wo, bo,
                 for cb in range(CB):
                     nc.tensor.transpose(vectors_ps[:, cb, :], rows[:, cb * P : (cb + 1) * P], ident_f32[:])
                 nc.vector.tensor_copy(vectors[:], vectors_ps[:, :, 0:4])
-            bq_scaled = held.tile([P, CB], F32, name="bq_scaled")
-            nc.vector.tensor_scalar_mul(bq_scaled[:], vectors[:, :, BQ], INV_SQRT_DH)
 
             ident = held.tile([P, P], BF16, name="ident")
             make_identity(nc, ident[:])
@@ -96,13 +95,15 @@ def tile_captioningtransformer_b_kernel(tc, emb, pe, wq, bq, wk, wv, bv, wo, bo,
                 compare_op=ALU.is_ge,
                 fill=MASKED,
                 base=0,
-                pattern=[[-1, P]],
-                channel_multiplier=1,
+                pattern=[[1, P]],
+                channel_multiplier=-1,
             )
             mask = held.tile([P, P], BF16, name="mask")
             nc.vector.tensor_copy(mask[:], mask_f32[:])
             averager = held.tile([P, P], BF16, name="averager")
             nc.vector.memset(averager[:], 1.0 / C)
+            ones = held.tile([P, P], BF16, name="ones")
+            nc.vector.memset(ones[:], 1.0)
             eps = held.tile([P, 1], F32, name="eps")
             nc.vector.memset(eps[:], EPS)
 
@@ -129,13 +130,11 @@ def tile_captioningtransformer_b_kernel(tc, emb, pe, wq, bq, wk, wv, bv, wo, bo,
                 for b in range(1, B):
                     look_up(cb, b)
 
-        block = ctx.enter_context(tc.tile_pool(name="block", bufs=6))
-        flipped = ctx.enter_context(tc.tile_pool(name="flipped", bufs=3))
         norm = ctx.enter_context(tc.tile_pool(name="norm", bufs=2))
         acc = ctx.enter_context(tc.psum_pool(name="acc", bufs=3))
         rare = ctx.enter_context(tc.psum_pool(name="rare", bufs=1))
         score = ctx.enter_context(tc.psum_pool(name="score", bufs=2))
-        flip = ctx.enter_context(tc.psum_pool(name="flip", bufs=2))
+        summed = ctx.enter_context(tc.psum_pool(name="summed", bufs=1))
 
         def project_qk(b):
             entries = slice(b * T, (b + 1) * T)
@@ -160,34 +159,28 @@ def tile_captioningtransformer_b_kernel(tc, emb, pe, wq, bq, wk, wv, bv, wo, bo,
 
         def attend(b, h):
             head = slice(h * P, (h + 1) * P)
-            pT_bf = flipped.tile([P, TB, T], BF16, name="pT_bf")
-            for jb in range(TB):
-                width = (jb + 1) * P
-                queries = slice(jb * P, width)
-                s_ps = score.tile([P, T], F32, name="s_ps")
-                nc.tensor.matmul(s_ps[:, :width], q_bf[b][:, h, queries], k_bf[b][:, h, :width], start=True, stop=False)
-                nc.tensor.matmul(s_ps[:, queries], ident[:], mask[:], start=False, stop=True)
-
-                minus_max = block.tile([P, 1], F32, name="minus_max")
-                nc.vector.reduce_max(minus_max[:], s_ps[:, :width], axis=mybir.AxisListType.X, negate=True)
-                e = block.tile([P, T], F32, name="e")
-                e_sum = block.tile([P, 1], F32, name="e_sum")
-                nc.scalar.activation(e[:, :width], s_ps[:, :width], FUNC.Exp, bias=minus_max[:], accum_out=e_sum[:])
-                inv_sum = block.tile([P, 1], F32, name="inv_sum")
-                nc.vector.reciprocal(inv_sum[:], e_sum[:])
-                p_bf = block.tile([P, T], BF16, name="p_bf")
-                nc.vector.tensor_scalar_mul(p_bf[:, :width], e[:, :width], inv_sum[:])
-
-                pT_ps = flip.tile([P, TB, P], BF16, name="pT_ps")
-                for ib in range(jb + 1):
-                    nc.tensor.transpose(pT_ps[:, ib, :], p_bf[:, ib * P : (ib + 1) * P], ident[:])
-                nc.vector.tensor_copy(pT_bf[:, : jb + 1, queries], pT_ps[:, : jb + 1, :])
-            y_ps = rare.tile([P, T], F32, name="y_ps", tag="rare")
+            e_bf = softmax.tile([P, TB, T], BF16, name="e_bf")
             for ib in range(TB):
+                first = ib * P
+                s_ps = score.tile([P, T], F32, name="s_ps")
                 nc.tensor.matmul(
-                    y_ps[:, ib * P :], vT_bf[b][:, ib, head], pT_bf[:, ib, ib * P :], start=ib == 0, stop=ib == TB - 1
+                    s_ps[:, first:], k_bf[b][:, h, first : first + P], q_bf[b][:, h, first:], start=True, stop=False
                 )
-            nc.scalar.copy(y_bf[b][:, h, :], y_ps[:])
+                nc.tensor.matmul(s_ps[:, first : first + P], ident[:], mask[:], start=False, stop=True)
+                nc.scalar.activation(e_bf[:, ib, first:], s_ps[:, first:], FUNC.Exp, scale=INV_SQRT_DH)
+            y_ps = summed.tile([P, T], F32, name="y_ps")
+            for ib in range(TB):
+                first = ib * P
+                nc.tensor.matmul(
+                    y_ps[:, first:], vT_bf[b][:, ib, head], e_bf[:, ib, first:], start=ib == 0, stop=ib == TB - 1
+                )
+            sum_ps = summed.tile([P, T], F32, name="sum_ps")
+            for ib in range(TB):
+                first = ib * P
+                nc.tensor.matmul(sum_ps[:, first:], ones[:], e_bf[:, ib, first:], start=ib == 0, stop=ib == TB - 1)
+            inv_sum = softmax.tile([P, T], F32, name="inv_sum")
+            nc.vector.reciprocal(inv_sum[:], sum_ps[:])
+            nc.vector.tensor_tensor(y_bf[b][:, h, :], y_ps[:], inv_sum[:], ALU.mult)
 
         def mean_over_features(blocks, name):
             partial = norm.tile([P, T], F32, name="partial")

@@ -17,6 +17,7 @@ TB = T // P
 EPS = 1e-5
 INV_SQRT_DH = 1.0 / math.sqrt(P)
 MASKED = -1e30
+VW = 144
 ROWS = 64
 BO, BQ, LN_W, LN_B = 0, 1, 2, 3
 
@@ -40,14 +41,15 @@ def tile_captioningtransformer_b_kernel(tc, emb, pe, wq, bq, wk, wv, bv, wo, bo,
         def new_caption(b):
             q_bf[b] = caption.tile([P, H, T], BF16, name="q_bf")
             k_bf[b] = caption.tile([P, H, T], BF16, name="k_bf")
-            vT_bf[b] = caption.tile([P, TB, C], BF16, name="vT_bf")
+            vT_bf[b] = caption.tile([P, TB, H, VW], BF16, name="vT_bf")
+            nc.gpsimd.memset(vT_bf[b][:, :, :, P : P + 1], 1.0)
             y_bf[b] = caption.tile([P, H, T], BF16, name="y_bf")
 
         def store_q(b, h, q_ps):
             nc.scalar.activation(q_bf[b][:, h, :], q_ps[:], FUNC.Identity, bias=vectors[:, h, BQ : BQ + 1])
 
         def store_k(b, h, k_ps):
-            nc.scalar.copy(k_bf[b][:, h, :], k_ps[:])
+            nc.vector.tensor_copy(k_bf[b][:, h, :], k_ps[:])
 
         with tc.tile_pool(name="start", bufs=1) as start:
             rows = start.tile([ROWS, C], F32, name="rows")
@@ -102,8 +104,6 @@ def tile_captioningtransformer_b_kernel(tc, emb, pe, wq, bq, wk, wv, bv, wo, bo,
             nc.vector.tensor_copy(mask[:], mask_f32[:])
             averager = held.tile([P, P], BF16, name="averager")
             nc.vector.memset(averager[:], 1.0 / C)
-            ones = held.tile([P, P], BF16, name="ones")
-            nc.vector.memset(ones[:], 1.0)
             eps = held.tile([P, 1], F32, name="eps")
             nc.vector.memset(eps[:], EPS)
 
@@ -123,72 +123,98 @@ def tile_captioningtransformer_b_kernel(tc, emb, pe, wq, bq, wk, wv, bv, wo, bo,
                         head = slice(h * P, (h + 1) * P)
                         nc.tensor.matmul(q_ps[h][:], wq_sb[:, cb, head], x_bf[cb][:, :T], start=cb == 0, stop=cb == CB - 1)
                         nc.tensor.matmul(k_ps[h][:], wk_sb[:, cb, head], x_bf[cb][:, :T], start=cb == 0, stop=cb == CB - 1)
-                for h in range(H):
-                    store_q(0, h, q_ps[h])
-                    store_k(0, h, k_ps[h])
-            for cb in range(CB):
-                for b in range(1, B):
-                    look_up(cb, b)
+                    if cb == CB - 1:
+                        for h in range(H):
+                            store_q(0, h, q_ps[h])
+                            store_k(0, h, k_ps[h])
+                    for b in range(1, B):
+                        look_up(cb, b)
 
         norm = ctx.enter_context(tc.tile_pool(name="norm", bufs=2))
+        leaving = ctx.enter_context(tc.tile_pool(name="leaving", bufs=4))
         acc = ctx.enter_context(tc.psum_pool(name="acc", bufs=3))
-        rare = ctx.enter_context(tc.psum_pool(name="rare", bufs=1))
         score = ctx.enter_context(tc.psum_pool(name="score", bufs=2))
-        summed = ctx.enter_context(tc.psum_pool(name="summed", bufs=1))
+        summed = ctx.enter_context(tc.psum_pool(name="summed", bufs=2))
+        flip = ctx.enter_context(tc.psum_pool(name="flip", bufs=1))
 
-        def project_qk(b):
-            entries = slice(b * T, (b + 1) * T)
-            for h in range(H):
-                head = slice(h * P, (h + 1) * P)
-                q_ps = acc.tile([P, T], F32, name="q_ps", tag="acc")
-                for cb in range(CB):
-                    nc.tensor.matmul(q_ps[:], wq_sb[:, cb, head], x_bf[cb][:, entries], start=cb == 0, stop=cb == CB - 1)
-                store_q(b, h, q_ps)
-                k_ps = acc.tile([P, T], F32, name="k_ps", tag="acc")
-                for cb in range(CB):
-                    nc.tensor.matmul(k_ps[:], wk_sb[:, cb, head], x_bf[cb][:, entries], start=cb == 0, stop=cb == CB - 1)
-                store_k(b, h, k_ps)
+        def project_q(b, h):
+            q_ps = acc.tile([P, T], F32, name="q_ps", tag="acc")
+            for cb in range(CB):
+                nc.tensor.matmul(
+                    q_ps[:], wq_sb[:, cb, h * P : (h + 1) * P], x_bf[cb][:, b * T : (b + 1) * T], start=cb == 0, stop=cb == CB - 1
+                )
+            store_q(b, h, q_ps)
 
-        def project_v(b):
-            for ib in range(TB):
-                keys = slice(b * T + ib * P, b * T + (ib + 1) * P)
-                v_ps = acc.tile([P, C], F32, name="v_ps", tag="acc")
-                for cb in range(CB):
-                    nc.tensor.matmul(v_ps[:], x_bf[cb][:, keys], wv_sb[:, cb, :], start=cb == 0, stop=cb == CB - 1)
-                nc.vector.tensor_tensor(vT_bf[b][:, ib, :], v_ps[:], bv_rows[:], ALU.add)
+        def project_k(b, h):
+            k_ps = acc.tile([P, T], F32, name="k_ps", tag="acc")
+            for cb in range(CB):
+                nc.tensor.matmul(
+                    k_ps[:], wk_sb[:, cb, h * P : (h + 1) * P], x_bf[cb][:, b * T : (b + 1) * T], start=cb == 0, stop=cb == CB - 1
+                )
+            store_k(b, h, k_ps)
 
-        def attend(b, h):
-            head = slice(h * P, (h + 1) * P)
-            e_bf = softmax.tile([P, TB, T], BF16, name="e_bf")
-            for ib in range(TB):
+        def project_v(b, ib):
+            keys = slice(b * T + ib * P, b * T + (ib + 1) * P)
+            v_ps = acc.tile([P, C], F32, name="v_ps", tag="acc")
+            for cb in range(CB):
+                nc.tensor.matmul(v_ps[:], x_bf[cb][:, keys], wv_sb[:, cb, :], start=cb == 0, stop=cb == CB - 1)
+            nc.vector.tensor_tensor(
+                vT_bf[b][:, ib, :, :P],
+                v_ps[:].rearrange("p (h d) -> p h d", h=H),
+                bv_rows[:].rearrange("p (h d) -> p h d", h=H),
+                ALU.add,
+            )
+
+        e_bf, yT_bf = {}, {}
+
+        def scores(b, h, key_blocks):
+            if (b, h) not in e_bf:
+                e_bf[b, h] = softmax.tile([P, TB, T], BF16, name="e_bf")
+            for ib in key_blocks:
                 first = ib * P
                 s_ps = score.tile([P, T], F32, name="s_ps")
                 nc.tensor.matmul(
-                    s_ps[:, first:], k_bf[b][:, h, first : first + P], q_bf[b][:, h, first:], start=True, stop=False
+                    s_ps[:, : T - first], k_bf[b][:, h, first : first + P], q_bf[b][:, h, first:], start=True, stop=False
                 )
-                nc.tensor.matmul(s_ps[:, first : first + P], ident[:], mask[:], start=False, stop=True)
-                nc.scalar.activation(e_bf[:, ib, first:], s_ps[:, first:], FUNC.Exp, scale=INV_SQRT_DH)
-            y_ps = summed.tile([P, T], F32, name="y_ps")
-            for ib in range(TB):
-                first = ib * P
-                nc.tensor.matmul(
-                    y_ps[:, first:], vT_bf[b][:, ib, head], e_bf[:, ib, first:], start=ib == 0, stop=ib == TB - 1
-                )
-            sum_ps = summed.tile([P, T], F32, name="sum_ps")
-            for ib in range(TB):
-                first = ib * P
-                nc.tensor.matmul(sum_ps[:, first:], ones[:], e_bf[:, ib, first:], start=ib == 0, stop=ib == TB - 1)
-            inv_sum = softmax.tile([P, T], F32, name="inv_sum")
-            nc.vector.reciprocal(inv_sum[:], sum_ps[:])
-            nc.vector.tensor_tensor(y_bf[b][:, h, :], y_ps[:], inv_sum[:], ALU.mult)
+                nc.tensor.matmul(s_ps[:, :P], ident[:], mask[:], start=False, stop=True)
+                nc.scalar.activation(e_bf[b, h][:, ib, : T - first], s_ps[:, : T - first], FUNC.Exp, scale=INV_SQRT_DH)
 
-        def mean_over_features(blocks, name):
+        def weigh(b, h, pair):
+            if (b, h) not in yT_bf:
+                yT_bf[b, h] = softmax.tile([P, TB, P], BF16, name="yT_bf")
+            yT_ps = summed.tile([P, 2, T // 2], F32, name="yT_ps")
+            for half in range(2):
+                jb = 2 * pair + half
+                for ib in range(jb + 1):
+                    nc.tensor.matmul(
+                        yT_ps[:, half, : P + 1],
+                        e_bf[b, h][:, ib, (jb - ib) * P : (jb - ib + 1) * P],
+                        vT_bf[b][:, ib, h, : P + 1],
+                        start=ib == 0,
+                        stop=ib == jb,
+                    )
+            inv_sum = softmax.tile([P, 2, 1], F32, name="inv_sum")
+            nc.vector.reciprocal(inv_sum[:], yT_ps[:, :, P : P + 1])
+            nc.vector.tensor_tensor(
+                yT_bf[b, h][:, 2 * pair : 2 * pair + 2, :], yT_ps[:, :, :P], inv_sum[:].to_broadcast([P, 2, P]), ALU.mult
+            )
+
+        def turn_back(b, h):
+            y_ps = flip.tile([P, T], BF16, name="y_ps")
+            for jb in range(TB):
+                nc.tensor.transpose(y_ps[:, jb * P : (jb + 1) * P], yT_bf[b, h][:, jb, :], ident[:])
+            nc.scalar.copy(y_bf[b][:, h, :], y_ps[:])
+
+        def add_blocks(blocks):
             partial = norm.tile([P, T], F32, name="partial")
             nc.gpsimd.tensor_tensor(partial[:], blocks[0], blocks[1], ALU.add)
             nc.gpsimd.tensor_tensor(partial[:], partial[:], blocks[2], ALU.add)
             partial_bf = norm.tile([P, T], BF16, name="partial_bf")
             nc.vector.tensor_tensor(partial_bf[:], partial[:], blocks[3], ALU.add)
-            mean_ps = rare.tile([P, T], F32, name=name, tag="rare")
+            return partial_bf
+
+        def average(partial_bf, name):
+            mean_ps = acc.tile([P, T], F32, name=name, tag="acc")
             nc.tensor.matmul(mean_ps[:], averager[:], partial_bf[:], start=True, stop=True)
             return mean_ps
 
@@ -199,54 +225,75 @@ def tile_captioningtransformer_b_kernel(tc, emb, pe, wq, bq, wk, wv, bv, wo, bo,
         for cb in range(CB):
             nc.vector.tensor_scalar_add(wo_centred[:, cb, :], wo_sb[:, cb, :], wo_shift[:, cb : cb + 1])
 
+        x_sum, centred, squares, square_sum, var_ps, inv_std = {}, {}, {}, {}, {}, {}
+
         def centre_x(b):
             entries = slice(b * T, (b + 1) * T)
-            mean_ps = mean_over_features([x[cb][:, entries] for cb in range(CB)], "mean_ps")
+            mean_ps = average(x_sum[b], "mean_ps")
             for cb in range(CB):
                 nc.vector.tensor_tensor(x[cb][:, entries], x[cb][:, entries], mean_ps[:], ALU.subtract)
 
-        def finish(b):
-            entries = slice(b * T, (b + 1) * T)
-            centred = norm.tile([P, CB, T], F32, name="centred")
-            squares = norm.tile([P, CB, T], F32, name="squares")
-            for mb in range(CB):
-                z_ps = acc.tile([P, T], F32, name="z_ps", tag="acc")
-                for cb in range(CB):
-                    nc.tensor.matmul(
-                        z_ps[:], wo_centred[:, cb, mb * P : (mb + 1) * P], y_bf[b][:, cb, :], start=cb == 0, stop=cb == CB - 1
-                    )
-                nc.vector.scalar_tensor_tensor(
-                    centred[:, mb, :], z_ps[:], vectors[:, mb, BO : BO + 1], x[mb][:, entries], ALU.add, ALU.add
+        def output_block(b, mb):
+            if b not in centred:
+                centred[b] = norm.tile([P, CB, T], F32, name="centred")
+                squares[b] = norm.tile([P, CB, T], F32, name="squares")
+            z_ps = acc.tile([P, T], F32, name="z_ps", tag="acc")
+            for cb in range(CB):
+                nc.tensor.matmul(
+                    z_ps[:], wo_centred[:, cb, mb * P : (mb + 1) * P], y_bf[b][:, cb, :], start=cb == 0, stop=cb == CB - 1
                 )
-                nc.scalar.square(squares[:, mb, :], centred[:, mb, :])
-            var_ps = mean_over_features([squares[:, mb, :] for mb in range(CB)], "var_ps")
+            nc.vector.scalar_tensor_tensor(
+                centred[b][:, mb, :], z_ps[:], vectors[:, mb, BO : BO + 1], x[mb][:, b * T : (b + 1) * T], ALU.add, ALU.add
+            )
+            nc.scalar.square(squares[b][:, mb, :], centred[b][:, mb, :])
 
-            inv_std = norm.tile([P, T], F32, name="inv_std")
-            nc.scalar.activation(inv_std[:], var_ps[:], FUNC.Abs_reciprocal_sqrt, bias=eps[:])
+        def normalise_block(b, mb):
+            normed = leaving.tile([P, T], F32, name="normed")
+            nc.vector.tensor_tensor(normed[:], centred[b][:, mb, :], inv_std[b][:], ALU.mult)
+            result = leaving.tile([P, T], F32, name="result")
+            nc.vector.tensor_scalar(
+                result[:], normed[:], vectors[:, mb, LN_W : LN_W + 1], vectors[:, mb, LN_B : LN_B + 1], ALU.mult, ALU.add
+            )
+            nc.sync.dma_start(out[mb * P : (mb + 1) * P, b * T : (b + 1) * T], result[:])
 
-            normed = norm.tile([P, CB, T], F32, name="normed")
-            result = norm.tile([P, CB, T], F32, name="result")
-            for mb in range(CB):
-                nc.vector.tensor_tensor(normed[:, mb, :], centred[:, mb, :], inv_std[:], ALU.mult)
-                nc.scalar.activation(
-                    result[:, mb, :],
-                    normed[:, mb, :],
-                    FUNC.Identity,
-                    bias=vectors[:, mb, LN_B : LN_B + 1],
-                    scale=vectors[:, mb, LN_W : LN_W + 1],
-                )
-                nc.sync.dma_start(out[mb * P : (mb + 1) * P, entries], result[:, mb, :])
-
-        project_v(0)
-        for b in range(B):
-            centre_x(b)
-        for b in range(B):
-            for h in range(H):
-                attend(b, h)
-            if b + 1 < B:
+        Z_LAG = H + 1
+        N_LAG = Z_LAG + CB
+        for ib in range(TB):
+            project_v(0, ib)
+        for step in range(B * H + N_LAG):
+            b, h = divmod(step, H)
+            zb, z_mb = divmod(step - Z_LAG, CB)
+            nb, n_mb = divmod(step - N_LAG, CB)
+            if h == 0 and b + 1 < B:
                 new_caption(b + 1)
-                project_qk(b + 1)
-                project_v(b + 1)
-            if b >= 1:
-                finish(b - 1)
-        finish(B - 1)
+            if h == 0 and b < B:
+                x_sum[b] = add_blocks([x[cb][:, b * T : (b + 1) * T] for cb in range(CB)])
+            if b < B:
+                scores(b, h, (0, 1))
+            if b + 1 < B:
+                project_q(b + 1, h)
+            if 2 <= step < B * H + 2:
+                turn_back((step - 2) // H, (step - 2) % H)
+            if nb >= 0 and n_mb == 0:
+                var_ps[nb] = average(square_sum[nb], "var_ps")
+            if b < B:
+                scores(b, h, (2, 3))
+            if nb >= 0 and n_mb == 0:
+                inv_std[nb] = norm.tile([P, T], F32, name="inv_std")
+                nc.scalar.activation(inv_std[nb][:], var_ps[nb][:], FUNC.Abs_reciprocal_sqrt, bias=eps[:])
+            if b + 1 < B:
+                project_k(b + 1, h)
+            if 1 <= step < B * H + 1:
+                weigh((step - 1) // H, (step - 1) % H, 0)
+            if b + 1 < B:
+                project_v(b + 1, h)
+            if 1 <= step < B * H + 1:
+                weigh((step - 1) // H, (step - 1) % H, 1)
+            if h == 1 and b < B:
+                centre_x(b)
+            if 0 <= zb < B:
+                output_block(zb, z_mb)
+                if z_mb == CB - 1:
+                    square_sum[zb] = add_blocks([squares[zb][:, i, :] for i in range(CB)])
+            if nb >= 0:
+                normalise_block(nb, n_mb)

@@ -16,7 +16,6 @@ CB = C // P
 TB = T // P
 EPS = 1e-5
 INV_SQRT_DH = 1.0 / math.sqrt(P)
-MASKED = -1e30
 VW = 144
 ROWS = 64
 BO, BQ, LN_W, LN_B = 0, 1, 2, 3
@@ -90,18 +89,18 @@ def tile_captioningtransformer_b_kernel(tc, emb, pe, wq, bq, wk, wv, bv, wo, bo,
             ident = held.tile([P, P], BF16, name="ident")
             make_identity(nc, ident[:])
             mask_f32 = start.tile([P, P], F32, name="mask_f32")
-            nc.gpsimd.memset(mask_f32[:], 0.0)
+            nc.gpsimd.memset(mask_f32[:], 1.0)
             nc.gpsimd.affine_select(
                 out=mask_f32[:],
                 in_=mask_f32[:],
                 compare_op=ALU.is_ge,
-                fill=MASKED,
+                fill=0.0,
                 base=0,
                 pattern=[[1, P]],
                 channel_multiplier=-1,
             )
-            mask = held.tile([P, P], BF16, name="mask")
-            nc.vector.tensor_copy(mask[:], mask_f32[:])
+            mask = held.tile([P, 1, P], BF16, name="mask")
+            nc.vector.tensor_copy(mask[:, 0, :], mask_f32[:])
             averager = held.tile([P, P], BF16, name="averager")
             nc.vector.memset(averager[:], 1.0 / C)
             eps = held.tile([P, 1], F32, name="eps")
@@ -174,10 +173,11 @@ def tile_captioningtransformer_b_kernel(tc, emb, pe, wq, bq, wk, wv, bv, wo, bo,
                 first = ib * P
                 s_ps = score.tile([P, T], F32, name="s_ps")
                 nc.tensor.matmul(
-                    s_ps[:, : T - first], k_bf[b][:, h, first : first + P], q_bf[b][:, h, first:], start=True, stop=False
+                    s_ps[:, : T - first], k_bf[b][:, h, first : first + P], q_bf[b][:, h, first:], start=True, stop=True
                 )
-                nc.tensor.matmul(s_ps[:, :P], ident[:], mask[:], start=False, stop=True)
                 nc.scalar.activation(e_bf[b, h][:, ib, : T - first], s_ps[:, : T - first], FUNC.Exp, scale=INV_SQRT_DH)
+            diagonal = e_bf[b, h][:, key_blocks[0] : key_blocks[-1] + 1, :P]
+            nc.vector.tensor_tensor(diagonal, diagonal, mask[:].to_broadcast([P, len(key_blocks), P]), ALU.mult)
 
         def weigh(b, h, pair):
             if (b, h) not in yT_bf:

@@ -129,8 +129,9 @@ def tile_captioningtransformer_b_kernel(tc, emb, pe, wq, bq, wk, wv, bv, wo, bo,
                     for b in range(1, B):
                         look_up(cb, b)
 
-        norm = ctx.enter_context(tc.tile_pool(name="norm", bufs=2))
+        norm = ctx.enter_context(tc.tile_pool(name="norm", bufs=3))
         leaving = ctx.enter_context(tc.tile_pool(name="leaving", bufs=4))
+        stored = ctx.enter_context(tc.tile_pool(name="stored", bufs=8))
         acc = ctx.enter_context(tc.psum_pool(name="acc", bufs=3))
         score = ctx.enter_context(tc.psum_pool(name="score", bufs=2))
         summed = ctx.enter_context(tc.psum_pool(name="summed", bufs=2))
@@ -225,7 +226,7 @@ def tile_captioningtransformer_b_kernel(tc, emb, pe, wq, bq, wk, wv, bv, wo, bo,
         for cb in range(CB):
             nc.vector.tensor_scalar_add(wo_centred[:, cb, :], wo_sb[:, cb, :], wo_shift[:, cb : cb + 1])
 
-        x_sum, centred, squares, square_sum, var_ps, inv_std = {}, {}, {}, {}, {}, {}
+        x_sum, centred, squares, square_sum, inv_std = {}, {}, {}, {}, {}
 
         def centre_x(b):
             entries = slice(b * T, (b + 1) * T)
@@ -250,17 +251,28 @@ def tile_captioningtransformer_b_kernel(tc, emb, pe, wq, bq, wk, wv, bv, wo, bo,
         def normalise_block(b, mb):
             normed = leaving.tile([P, T], F32, name="normed")
             nc.vector.tensor_tensor(normed[:], centred[b][:, mb, :], inv_std[b][:], ALU.mult)
-            result = leaving.tile([P, T], F32, name="result")
-            nc.vector.tensor_scalar(
-                result[:], normed[:], vectors[:, mb, LN_W : LN_W + 1], vectors[:, mb, LN_B : LN_B + 1], ALU.mult, ALU.add
+            result = stored.tile([P, T], F32, name="result")
+            nc.scalar.activation(
+                result[:],
+                normed[:],
+                FUNC.Identity,
+                bias=vectors[:, mb, LN_B : LN_B + 1],
+                scale=vectors[:, mb, LN_W : LN_W + 1],
             )
             nc.sync.dma_start(out[mb * P : (mb + 1) * P, b * T : (b + 1) * T], result[:])
 
+        def deviation(b, pool, tag):
+            var_ps = pool.tile([P, T], F32, name="var_ps", tag=tag)
+            nc.tensor.matmul(var_ps[:], averager[:], square_sum[b][:], start=True, stop=True)
+            inv_std[b] = norm.tile([P, T], F32, name="inv_std")
+            nc.scalar.activation(inv_std[b][:], var_ps[:], FUNC.Abs_reciprocal_sqrt, bias=eps[:])
+
         Z_LAG = H + 1
         N_LAG = Z_LAG + CB
+        STEPS = B * H
         for ib in range(TB):
             project_v(0, ib)
-        for step in range(B * H + N_LAG):
+        for step in range(STEPS + 2):
             b, h = divmod(step, H)
             zb, z_mb = divmod(step - Z_LAG, CB)
             nb, n_mb = divmod(step - N_LAG, CB)
@@ -272,28 +284,36 @@ def tile_captioningtransformer_b_kernel(tc, emb, pe, wq, bq, wk, wv, bv, wo, bo,
                 scores(b, h, (0, 1))
             if b + 1 < B:
                 project_q(b + 1, h)
-            if 2 <= step < B * H + 2:
+            if step >= 2:
                 turn_back((step - 2) // H, (step - 2) % H)
-            if nb >= 0 and n_mb == 0:
-                var_ps[nb] = average(square_sum[nb], "var_ps")
             if b < B:
                 scores(b, h, (2, 3))
-            if nb >= 0 and n_mb == 0:
-                inv_std[nb] = norm.tile([P, T], F32, name="inv_std")
-                nc.scalar.activation(inv_std[nb][:], var_ps[nb][:], FUNC.Abs_reciprocal_sqrt, bias=eps[:])
+            if nb >= 0 and n_mb == 0 and b + 1 < B:
+                deviation(nb, acc, "acc")
             if b + 1 < B:
                 project_k(b + 1, h)
-            if 1 <= step < B * H + 1:
+            if 1 <= step <= STEPS:
                 weigh((step - 1) // H, (step - 1) % H, 0)
             if b + 1 < B:
                 project_v(b + 1, h)
-            if 1 <= step < B * H + 1:
+            if 1 <= step <= STEPS:
                 weigh((step - 1) // H, (step - 1) % H, 1)
             if h == 1 and b < B:
                 centre_x(b)
-            if 0 <= zb < B:
+            if 0 <= zb < B - 1:
                 output_block(zb, z_mb)
                 if z_mb == CB - 1:
                     square_sum[zb] = add_blocks([squares[zb][:, i, :] for i in range(CB)])
-            if nb >= 0:
+            if nb in inv_std:
                 normalise_block(nb, n_mb)
+
+        waiting = [nb for nb in range(B - 1) if nb not in inv_std]
+        for nb in waiting:
+            deviation(nb, score, "s_ps")
+        for mb in range(CB):
+            output_block(B - 1, mb)
+        square_sum[B - 1] = add_blocks([squares[B - 1][:, i, :] for i in range(CB)])
+        deviation(B - 1, acc, "acc")
+        for nb in waiting + [B - 1]:
+            for mb in range(CB):
+                normalise_block(nb, mb)

@@ -28,7 +28,7 @@ def tile_captioningtransformer_b_kernel(tc, emb, pe, wq, bq, wk, wv, bv, wo, bo,
     with ExitStack() as ctx:
         held = ctx.enter_context(tc.tile_pool(name="held", bufs=1))
         caption = ctx.enter_context(tc.tile_pool(name="caption", bufs=3))
-        softmax = ctx.enter_context(tc.tile_pool(name="softmax", bufs=3))
+        softmax = ctx.enter_context(tc.tile_pool(name="softmax", bufs=4))
 
         offsets = held.tile([P, N // 16], U16, name="offsets")
         nc.sync.dma_start(offsets[:], offs)
@@ -267,12 +267,12 @@ def tile_captioningtransformer_b_kernel(tc, emb, pe, wq, bq, wk, wv, bv, wo, bo,
             inv_std[b] = norm.tile([P, T], F32, name="inv_std")
             nc.scalar.activation(inv_std[b][:], var_ps[:], FUNC.Abs_reciprocal_sqrt, bias=eps[:])
 
-        Z_LAG = H + 1
+        Z_LAG = H + 2
         N_LAG = Z_LAG + CB
         STEPS = B * H
         for ib in range(TB):
             project_v(0, ib)
-        for step in range(STEPS + 2):
+        for step in range(STEPS + 3):
             b, h = divmod(step, H)
             zb, z_mb = divmod(step - Z_LAG, CB)
             nb, n_mb = divmod(step - N_LAG, CB)
@@ -284,20 +284,20 @@ def tile_captioningtransformer_b_kernel(tc, emb, pe, wq, bq, wk, wv, bv, wo, bo,
                 scores(b, h, (0, 1))
             if b + 1 < B:
                 project_q(b + 1, h)
-            if step >= 2:
-                turn_back((step - 2) // H, (step - 2) % H)
+            if 3 <= step:
+                turn_back((step - 3) // H, (step - 3) % H)
+            if b + 1 < B:
+                project_k(b + 1, h)
             if b < B:
                 scores(b, h, (2, 3))
             if nb >= 0 and n_mb == 0 and b + 1 < B:
                 deviation(nb, acc, "acc")
-            if b + 1 < B:
-                project_k(b + 1, h)
-            if 1 <= step <= STEPS:
-                weigh((step - 1) // H, (step - 1) % H, 0)
+            if 2 <= step <= STEPS + 1:
+                weigh((step - 2) // H, (step - 2) % H, 0)
             if b + 1 < B:
                 project_v(b + 1, h)
-            if 1 <= step <= STEPS:
-                weigh((step - 1) // H, (step - 1) % H, 1)
+            if 2 <= step <= STEPS + 1:
+                weigh((step - 2) // H, (step - 2) % H, 1)
             if h == 1 and b < B:
                 centre_x(b)
             if 0 <= zb < B - 1:

@@ -231,8 +231,10 @@ def tile_captioningtransformer_b_kernel(tc, emb, pe, wq, bq, wk, wv, bv, wo, bo,
         def centre_x(b):
             entries = slice(b * T, (b + 1) * T)
             mean_ps = average(x_sum[b], "mean_ps")
+            mean = norm.tile([P, T], F32, name="mean")
+            nc.scalar.copy(mean[:], mean_ps[:])
             for cb in range(CB):
-                nc.vector.tensor_tensor(x[cb][:, entries], x[cb][:, entries], mean_ps[:], ALU.subtract)
+                nc.gpsimd.tensor_tensor(x[cb][:, entries], x[cb][:, entries], mean[:], ALU.subtract)
 
         def output_block(b, mb):
             if b not in centred:

@@ -35,7 +35,7 @@ def tile_captioningtransformer_b_kernel(tc, emb, pe, wq, bq, wk, wv, bv, wo, bo,
 
         x = [held.tile([P, N], F32, name=f"x{cb}") for cb in range(CB)]
         x_bf = [held.tile([P, N], BF16, name=f"x_bf{cb}") for cb in range(CB)]
-        q_bf, k_bf, vT_bf, y_bf = {}, {}, {}, {}
+        q_early, q_bf, k_bf, vT_bf, y_bf = {}, {}, {}, {}, {}
 
         def new_caption(b):
             q_bf[b] = caption.tile([P, H, T], BF16, name="q_bf")
@@ -44,27 +44,27 @@ def tile_captioningtransformer_b_kernel(tc, emb, pe, wq, bq, wk, wv, bv, wo, bo,
             nc.gpsimd.memset(vT_bf[b][:, :, :, P : P + 1], 1.0)
             y_bf[b] = caption.tile([P, H, T], BF16, name="y_bf")
 
-        def store_q(b, h, q_ps):
-            nc.scalar.activation(q_bf[b][:, h, :], q_ps[:], FUNC.Identity, bias=vectors[:, h, BQ : BQ + 1])
-
-        def store_k(b, h, k_ps):
-            nc.vector.tensor_copy(k_bf[b][:, h, :], k_ps[:])
+        norm = ctx.enter_context(tc.tile_pool(name="norm", bufs=3))
+        acc = ctx.enter_context(tc.psum_pool(name="acc", bufs=3))
+        score = ctx.enter_context(tc.psum_pool(name="score", bufs=2))
+        summed = ctx.enter_context(tc.psum_pool(name="summed", bufs=2))
+        flip = ctx.enter_context(tc.psum_pool(name="flip", bufs=1))
 
         with tc.tile_pool(name="start", bufs=1) as start:
             rows = start.tile([ROWS, C], F32, name="rows")
             nc.vector.memset(rows[:], 0.0)
             for r, vector in ((BO, bo), (BQ, bq), (LN_W, ln_w), (LN_B, ln_b)):
                 nc.sync.dma_start(rows[r : r + 1, :], vector.rearrange("c one -> one c"))
-            pos = start.tile([P, CB, T], F32, name="pos")
-            nc.sync.dma_start(pos[:], pe.rearrange("(cb p) t -> p cb t", p=P))
+            pos = [start.tile([P, T], F32, name=f"pos{cb}") for cb in range(CB)]
             table = [start.tile([P, S], F32, name=f"table{cb}") for cb in range(CB)]
-            nc.sync.dma_start(table[0][:], emb[0:P, :])
             wq_sb = held.tile([P, CB, C], BF16, name="wq_sb")
-            nc.sync.dma_start(wq_sb[:], wq.rearrange("(cb p) m -> p cb m", p=P))
+            for cb in range(CB):
+                nc.sync.dma_start(pos[cb][:], pe[cb * P : (cb + 1) * P, :])
+                nc.sync.dma_start(table[cb][:], emb[cb * P : (cb + 1) * P, :])
+                if cb == 0:
+                    nc.sync.dma_start(wq_sb[:], wq.rearrange("(cb p) m -> p cb m", p=P))
             wk_sb = held.tile([P, CB, C], BF16, name="wk_sb")
             nc.sync.dma_start(wk_sb[:], wk.rearrange("(cb p) m -> p cb m", p=P))
-            for cb in range(1, CB):
-                nc.sync.dma_start(table[cb][:], emb[cb * P : (cb + 1) * P, :])
             wv_sb = held.tile([P, CB, C], BF16, name="wv_sb")
             nc.sync.dma_start(wv_sb[:], wv.rearrange("(cb p) m -> p cb m", p=P))
             bv_rows = held.tile([P, C], F32, name="bv_rows")
@@ -80,11 +80,10 @@ def tile_captioningtransformer_b_kernel(tc, emb, pe, wq, bq, wk, wv, bv, wo, bo,
             ident_f32 = start.tile([ROWS, ROWS], F32, name="ident_f32")
             make_identity(nc, ident_f32[:])
             vectors = held.tile([P, CB, 4], F32, name="vectors")
-            with tc.psum_pool(name="turned", bufs=1) as turned:
-                vectors_ps = turned.tile([P, CB, ROWS], F32, name="vectors_ps")
-                for cb in range(CB):
-                    nc.tensor.transpose(vectors_ps[:, cb, :], rows[:, cb * P : (cb + 1) * P], ident_f32[:])
-                nc.vector.tensor_copy(vectors[:], vectors_ps[:, :, 0:4])
+            vectors_ps = flip.tile([P, CB, ROWS], F32, name="vectors_ps", tag="y_ps")
+            for cb in range(CB):
+                nc.tensor.transpose(vectors_ps[:, cb, :], rows[:, cb * P : (cb + 1) * P], ident_f32[:])
+            nc.vector.tensor_copy(vectors[:], vectors_ps[:, :, 0:4])
 
             ident = held.tile([P, P], BF16, name="ident")
             make_identity(nc, ident[:])
@@ -109,41 +108,55 @@ def tile_captioningtransformer_b_kernel(tc, emb, pe, wq, bq, wk, wv, bv, wo, bo,
             def look_up(cb, b):
                 entries = slice(b * T, (b + 1) * T)
                 picked = table[cb][:].indirect(offsets[:, b * T // 16 : (b + 1) * T // 16])
-                nc.vector.tensor_tensor(x[cb][:, entries], picked, pos[:, cb, :], ALU.add)
+                nc.vector.tensor_tensor(x[cb][:, entries], picked, pos[cb][:], ALU.add)
                 nc.scalar.copy(x_bf[cb][:, entries], x[cb][:, entries])
 
-            new_caption(0)
-            with tc.psum_pool(name="first", bufs=1) as first:
-                q_ps = [first.tile([P, T], F32, name=f"q_ps{h}") for h in range(H)]
-                k_ps = [first.tile([P, T], F32, name=f"k_ps{h}") for h in range(H)]
-                for cb in range(CB):
-                    look_up(cb, 0)
-                    for h in range(H):
-                        head = slice(h * P, (h + 1) * P)
-                        nc.tensor.matmul(q_ps[h][:], wq_sb[:, cb, head], x_bf[cb][:, :T], start=cb == 0, stop=cb == CB - 1)
-                        nc.tensor.matmul(k_ps[h][:], wk_sb[:, cb, head], x_bf[cb][:, :T], start=cb == 0, stop=cb == CB - 1)
-                    if cb == CB - 1:
-                        for h in range(H):
-                            store_q(0, h, q_ps[h])
-                            store_k(0, h, k_ps[h])
-                    for b in range(1, B):
-                        look_up(cb, b)
+            def add_to_q(q_ps, b, h, cbs):
+                for cb in cbs:
+                    nc.tensor.matmul(
+                        q_ps[:],
+                        wq_sb[:, cb, h * P : (h + 1) * P],
+                        x_bf[cb][:, b * T : (b + 1) * T],
+                        start=cb == cbs[0],
+                        stop=cb == cbs[-1],
+                    )
 
-        norm = ctx.enter_context(tc.tile_pool(name="norm", bufs=3))
+            def sum_early(b):
+                q_early[b] = norm.tile([P, H, T], F32, name="q_early", tag="centred")
+                for h in range(H):
+                    early_ps = acc.tile([P, T], F32, name="early_ps", tag="acc")
+                    add_to_q(early_ps, b, h, range(b + 1))
+                    nc.scalar.activation(q_early[b][:, h, :], early_ps[:], FUNC.Identity, bias=vectors[:, h, BQ : BQ + 1])
+
+            new_caption(0)
+            q_ps = [score.tile([P, T], F32, name=f"q_ps{h}", tag="s_ps") for h in range(2)]
+            q_ps += [summed.tile([P, T], F32, name=f"q_ps{h}", tag="yT_ps") for h in range(2, 4)]
+            for cb in range(CB):
+                look_up(cb, 0)
+                for h in range(H):
+                    nc.tensor.matmul(
+                        q_ps[h][:], wq_sb[:, cb, h * P : (h + 1) * P], x_bf[cb][:, :T], start=cb == 0, stop=cb == CB - 1
+                    )
+                if cb == CB - 1:
+                    for h in range(H):
+                        nc.scalar.activation(q_bf[0][:, h, :], q_ps[h][:], FUNC.Identity, bias=vectors[:, h, BQ : BQ + 1])
+                if cb >= 2:
+                    sum_early(cb - 1)
+                for b in range(1, B):
+                    look_up(cb, b)
+
+        tail = ctx.enter_context(tc.tile_pool(name="tail", bufs=3))
         leaving = ctx.enter_context(tc.tile_pool(name="leaving", bufs=4))
         stored = ctx.enter_context(tc.tile_pool(name="stored", bufs=8))
-        acc = ctx.enter_context(tc.psum_pool(name="acc", bufs=3))
-        score = ctx.enter_context(tc.psum_pool(name="score", bufs=2))
-        summed = ctx.enter_context(tc.psum_pool(name="summed", bufs=2))
-        flip = ctx.enter_context(tc.psum_pool(name="flip", bufs=1))
 
         def project_q(b, h):
             q_ps = acc.tile([P, T], F32, name="q_ps", tag="acc")
-            for cb in range(CB):
-                nc.tensor.matmul(
-                    q_ps[:], wq_sb[:, cb, h * P : (h + 1) * P], x_bf[cb][:, b * T : (b + 1) * T], start=cb == 0, stop=cb == CB - 1
-                )
-            store_q(b, h, q_ps)
+            if b in q_early:
+                add_to_q(q_ps, b, h, range(b + 1, CB))
+                nc.vector.tensor_tensor(q_bf[b][:, h, :], q_ps[:], q_early[b][:, h, :], ALU.add)
+            else:
+                add_to_q(q_ps, b, h, range(CB))
+                nc.scalar.activation(q_bf[b][:, h, :], q_ps[:], FUNC.Identity, bias=vectors[:, h, BQ : BQ + 1])
 
         def project_k(b, h):
             k_ps = acc.tile([P, T], F32, name="k_ps", tag="acc")
@@ -151,7 +164,7 @@ def tile_captioningtransformer_b_kernel(tc, emb, pe, wq, bq, wk, wv, bv, wo, bo,
                 nc.tensor.matmul(
                     k_ps[:], wk_sb[:, cb, h * P : (h + 1) * P], x_bf[cb][:, b * T : (b + 1) * T], start=cb == 0, stop=cb == CB - 1
                 )
-            store_k(b, h, k_ps)
+            nc.vector.tensor_copy(k_bf[b][:, h, :], k_ps[:])
 
         def project_v(b, ib):
             keys = slice(b * T + ib * P, b * T + (ib + 1) * P)
@@ -207,10 +220,10 @@ def tile_captioningtransformer_b_kernel(tc, emb, pe, wq, bq, wk, wv, bv, wo, bo,
             nc.scalar.copy(y_bf[b][:, h, :], y_ps[:])
 
         def add_blocks(blocks):
-            partial = norm.tile([P, T], F32, name="partial")
+            partial = tail.tile([P, T], F32, name="partial")
             nc.gpsimd.tensor_tensor(partial[:], blocks[0], blocks[1], ALU.add)
             nc.gpsimd.tensor_tensor(partial[:], partial[:], blocks[2], ALU.add)
-            partial_bf = norm.tile([P, T], BF16, name="partial_bf")
+            partial_bf = tail.tile([P, T], BF16, name="partial_bf")
             nc.vector.tensor_tensor(partial_bf[:], partial[:], blocks[3], ALU.add)
             return partial_bf
 
@@ -219,19 +232,19 @@ def tile_captioningtransformer_b_kernel(tc, emb, pe, wq, bq, wk, wv, bv, wo, bo,
             nc.tensor.matmul(mean_ps[:], averager[:], partial_bf[:], start=True, stop=True)
             return mean_ps
 
-        wo_shift = held.tile([P, CB], F32, name="wo_shift")
-        nc.vector.reduce_sum(wo_shift[:], wo_sb[:], axis=mybir.AxisListType.X)
-        nc.vector.tensor_scalar_mul(wo_shift[:], wo_shift[:], -1.0 / C)
-        wo_centred = held.tile([P, CB, C], BF16, name="wo_centred")
-        for cb in range(CB):
-            nc.vector.tensor_scalar_add(wo_centred[:, cb, :], wo_sb[:, cb, :], wo_shift[:, cb : cb + 1])
+        def centre_wo():
+            wo_shift = held.tile([P, CB], F32, name="wo_shift")
+            for cb in range(CB):
+                nc.vector.reduce_sum(wo_shift[:, cb : cb + 1], wo_sb[:, cb, :], axis=mybir.AxisListType.X)
+                nc.vector.tensor_scalar_mul(wo_shift[:, cb : cb + 1], wo_shift[:, cb : cb + 1], -1.0 / C)
+                nc.vector.tensor_scalar_add(wo_sb[:, cb, :], wo_sb[:, cb, :], wo_shift[:, cb : cb + 1])
 
         x_sum, centred, squares, square_sum, inv_std = {}, {}, {}, {}, {}
 
         def centre_x(b):
             entries = slice(b * T, (b + 1) * T)
             mean_ps = average(x_sum[b], "mean_ps")
-            mean = norm.tile([P, T], F32, name="mean")
+            mean = tail.tile([P, T], F32, name="mean")
             nc.scalar.copy(mean[:], mean_ps[:])
             for cb in range(CB):
                 nc.gpsimd.tensor_tensor(x[cb][:, entries], x[cb][:, entries], mean[:], ALU.subtract)
@@ -239,11 +252,11 @@ def tile_captioningtransformer_b_kernel(tc, emb, pe, wq, bq, wk, wv, bv, wo, bo,
         def output_block(b, mb):
             if b not in centred:
                 centred[b] = norm.tile([P, CB, T], F32, name="centred")
-                squares[b] = norm.tile([P, CB, T], F32, name="squares")
+                squares[b] = tail.tile([P, CB, T], BF16 if b == B - 1 else F32, name="squares")
             z_ps = acc.tile([P, T], F32, name="z_ps", tag="acc")
             for cb in range(CB):
                 nc.tensor.matmul(
-                    z_ps[:], wo_centred[:, cb, mb * P : (mb + 1) * P], y_bf[b][:, cb, :], start=cb == 0, stop=cb == CB - 1
+                    z_ps[:], wo_sb[:, cb, mb * P : (mb + 1) * P], y_bf[b][:, cb, :], start=cb == 0, stop=cb == CB - 1
                 )
             nc.vector.scalar_tensor_tensor(
                 centred[b][:, mb, :], z_ps[:], vectors[:, mb, BO : BO + 1], x[mb][:, b * T : (b + 1) * T], ALU.add, ALU.add
@@ -263,44 +276,53 @@ def tile_captioningtransformer_b_kernel(tc, emb, pe, wq, bq, wk, wv, bv, wo, bo,
             )
             nc.sync.dma_start(out[mb * P : (mb + 1) * P, b * T : (b + 1) * T], result[:])
 
+        def store_deviation(b, var_ps):
+            inv_std[b] = tail.tile([P, T], F32, name="inv_std")
+            nc.scalar.activation(inv_std[b][:], var_ps[:], FUNC.Abs_reciprocal_sqrt, bias=eps[:])
+
         def deviation(b, pool, tag):
             var_ps = pool.tile([P, T], F32, name="var_ps", tag=tag)
             nc.tensor.matmul(var_ps[:], averager[:], square_sum[b][:], start=True, stop=True)
-            inv_std[b] = norm.tile([P, T], F32, name="inv_std")
-            nc.scalar.activation(inv_std[b][:], var_ps[:], FUNC.Abs_reciprocal_sqrt, bias=eps[:])
+            store_deviation(b, var_ps)
 
+        P_LEAD = 2
         Z_LAG = H + 2
         N_LAG = Z_LAG + CB
         STEPS = B * H
-        for ib in range(TB):
+        for h in range(P_LEAD):
+            project_k(0, h)
+        for ib in range(P_LEAD):
             project_v(0, ib)
         for step in range(STEPS + 3):
             b, h = divmod(step, H)
+            pb, ph = divmod(step + P_LEAD, H)
             zb, z_mb = divmod(step - Z_LAG, CB)
             nb, n_mb = divmod(step - N_LAG, CB)
-            if h == 0 and b + 1 < B:
-                new_caption(b + 1)
-            if h == 0 and b < B:
-                x_sum[b] = add_blocks([x[cb][:, b * T : (b + 1) * T] for cb in range(CB)])
+            if ph == 0 and 1 <= pb < B:
+                new_caption(pb)
             if b < B:
                 scores(b, h, (0, 1))
-            if b + 1 < B:
-                project_q(b + 1, h)
+            if 1 <= pb < B:
+                project_q(pb, ph)
             if 3 <= step:
                 turn_back((step - 3) // H, (step - 3) % H)
-            if b + 1 < B:
-                project_k(b + 1, h)
+            if pb < B:
+                project_k(pb, ph)
             if b < B:
                 scores(b, h, (2, 3))
             if nb >= 0 and n_mb == 0 and b + 1 < B:
                 deviation(nb, acc, "acc")
             if 2 <= step <= STEPS + 1:
                 weigh((step - 2) // H, (step - 2) % H, 0)
-            if b + 1 < B:
-                project_v(b + 1, h)
+            if pb < B:
+                project_v(pb, ph)
             if 2 <= step <= STEPS + 1:
                 weigh((step - 2) // H, (step - 2) % H, 1)
-            if h == 1 and b < B:
+            if step == Z_LAG - 1:
+                centre_wo()
+            if h == 2 and b < B:
+                x_sum[b] = add_blocks([x[cb][:, b * T : (b + 1) * T] for cb in range(CB)])
+            if h == 3 and b < B:
                 centre_x(b)
             if 0 <= zb < B - 1:
                 output_block(zb, z_mb)
@@ -312,10 +334,11 @@ def tile_captioningtransformer_b_kernel(tc, emb, pe, wq, bq, wk, wv, bv, wo, bo,
         waiting = [nb for nb in range(B - 1) if nb not in inv_std]
         for nb in waiting:
             deviation(nb, score, "s_ps")
+        var_ps = summed.tile([P, T], F32, name="var_ps", tag="yT_ps")
         for mb in range(CB):
             output_block(B - 1, mb)
-        square_sum[B - 1] = add_blocks([squares[B - 1][:, i, :] for i in range(CB)])
-        deviation(B - 1, acc, "acc")
+            nc.tensor.matmul(var_ps[:], averager[:], squares[B - 1][:, mb, :], start=mb == 0, stop=mb == CB - 1)
+        store_deviation(B - 1, var_ps)
         for nb in waiting + [B - 1]:
             for mb in range(CB):
                 normalise_block(nb, mb)

@@ -28,7 +28,7 @@ def tile_captioningtransformer_b_kernel(tc, emb, pe, wq, bq, wk, wv, bv, wo, bo,
     with ExitStack() as ctx:
         held = ctx.enter_context(tc.tile_pool(name="held", bufs=1))
         caption = ctx.enter_context(tc.tile_pool(name="caption", bufs=3))
-        softmax = ctx.enter_context(tc.tile_pool(name="softmax", bufs=4))
+        softmax = ctx.enter_context(tc.tile_pool(name="softmax", bufs=6))
 
         offsets = held.tile([P, N // 16], U16, name="offsets")
         nc.sync.dma_start(offsets[:], offs)
@@ -42,7 +42,7 @@ def tile_captioningtransformer_b_kernel(tc, emb, pe, wq, bq, wk, wv, bv, wo, bo,
             k_bf[b] = caption.tile([P, H, T], BF16, name="k_bf")
             vT_bf[b] = caption.tile([P, TB, H, VW], BF16, name="vT_bf")
             nc.gpsimd.memset(vT_bf[b][:, :, :, P : P + 1], 1.0)
-            y_bf[b] = caption.tile([P, H, T], BF16, name="y_bf")
+            y_bf[b] = caption.tile([P, H, 2, T // 2], BF16, name="y_bf")
 
         norm = ctx.enter_context(tc.tile_pool(name="norm", bufs=3))
         acc = ctx.enter_context(tc.psum_pool(name="acc", bufs=3))
@@ -53,8 +53,6 @@ def tile_captioningtransformer_b_kernel(tc, emb, pe, wq, bq, wk, wv, bv, wo, bo,
         with tc.tile_pool(name="start", bufs=1) as start:
             rows = start.tile([ROWS, C], F32, name="rows")
             nc.vector.memset(rows[:], 0.0)
-            for r, vector in ((BO, bo), (BQ, bq), (LN_W, ln_w), (LN_B, ln_b)):
-                nc.sync.dma_start(rows[r : r + 1, :], vector.rearrange("c one -> one c"))
             pos = [start.tile([P, T], F32, name=f"pos{cb}") for cb in range(CB)]
             table = [start.tile([P, S], F32, name=f"table{cb}") for cb in range(CB)]
             wq_sb = held.tile([P, CB, C], BF16, name="wq_sb")
@@ -63,6 +61,8 @@ def tile_captioningtransformer_b_kernel(tc, emb, pe, wq, bq, wk, wv, bv, wo, bo,
                 nc.sync.dma_start(table[cb][:], emb[cb * P : (cb + 1) * P, :])
                 if cb == 0:
                     nc.sync.dma_start(wq_sb[:], wq.rearrange("(cb p) m -> p cb m", p=P))
+                    for r, vector in ((BO, bo), (BQ, bq), (LN_W, ln_w), (LN_B, ln_b)):
+                        nc.sync.dma_start(rows[r : r + 1, :], vector.rearrange("c one -> one c"))
             wk_sb = held.tile([P, CB, C], BF16, name="wk_sb")
             nc.sync.dma_start(wk_sb[:], wk.rearrange("(cb p) m -> p cb m", p=P))
             wv_sb = held.tile([P, CB, C], BF16, name="wv_sb")
@@ -146,6 +146,8 @@ def tile_captioningtransformer_b_kernel(tc, emb, pe, wq, bq, wk, wv, bv, wo, bo,
                     look_up(cb, b)
 
         tail = ctx.enter_context(tc.tile_pool(name="tail", bufs=3))
+        squared = ctx.enter_context(tc.tile_pool(name="squared", bufs=2))
+        ending = ctx.enter_context(tc.tile_pool(name="ending", bufs=2))
         leaving = ctx.enter_context(tc.tile_pool(name="leaving", bufs=4))
         stored = ctx.enter_context(tc.tile_pool(name="stored", bufs=8))
 
@@ -178,53 +180,73 @@ def tile_captioningtransformer_b_kernel(tc, emb, pe, wq, bq, wk, wv, bv, wo, bo,
                 ALU.add,
             )
 
-        e_bf, yT_bf = {}, {}
+        e_bf, e_begin, yT_bf = {}, {}, {}
 
-        def scores(b, h, key_blocks):
-            if (b, h) not in e_bf:
-                e_bf[b, h] = softmax.tile([P, TB, T], BF16, name="e_bf")
-            for ib in key_blocks:
-                first = ib * P
-                s_ps = score.tile([P, T], F32, name="s_ps")
-                nc.tensor.matmul(
-                    s_ps[:, : T - first], k_bf[b][:, h, first : first + P], q_bf[b][:, h, first:], start=True, stop=True
-                )
-                nc.scalar.activation(e_bf[b, h][:, ib, : T - first], s_ps[:, : T - first], FUNC.Exp, scale=INV_SQRT_DH)
-            diagonal = e_bf[b, h][:, key_blocks[0] : key_blocks[-1] + 1, :P]
-            nc.vector.tensor_tensor(diagonal, diagonal, mask[:].to_broadcast([P, len(key_blocks), P]), ALU.mult)
+        def scores(b, h, queries, key_pairs):
+            head = (b, h, queries)
+            if head not in e_bf:
+                first, last = queries
+                begin = 0
+                for ib in range(last // P):
+                    e_begin[b, h, queries, ib] = begin
+                    begin += last - max(ib * P, first)
+                e_bf[head] = softmax.tile([P, begin + P], BF16, name="e_bf")
+            for pair in key_pairs:
+                banks = [(2 * pair, 2 * pair + 1)]
+                if queries[1] - queries[0] > T // 2 and pair == 0:
+                    banks = [(0,), (1,)]
+                for bank in banks:
+                    s_ps = score.tile([P, T], F32, name="s_ps")
+                    origin = e_begin[b, h, queries, bank[0]]
+                    for ib in bank:
+                        seen = slice(max(ib * P, queries[0]), queries[1])
+                        begin = e_begin[b, h, queries, ib] - origin
+                        end = begin + seen.stop - seen.start
+                        nc.tensor.matmul(
+                            s_ps[:, begin:end], k_bf[b][:, h, ib * P : (ib + 1) * P], q_bf[b][:, h, seen], start=True, stop=True
+                        )
+                    nc.scalar.activation(
+                        e_bf[head][:, origin : origin + end], s_ps[:, :end], FUNC.Exp, scale=INV_SQRT_DH
+                    )
+                if 2 * pair * P >= queries[0]:
+                    begin = e_begin[b, h, queries, 2 * pair]
+                    width = e_begin[b, h, queries, 2 * pair + 1] - begin
+                    diagonal = e_bf[head][:, begin : begin + 2 * width].rearrange("p (two q) -> p two q", two=2)[:, :, :P]
+                    nc.vector.tensor_tensor(diagonal, diagonal, mask[:].to_broadcast([P, 2, P]), ALU.mult)
 
-        def weigh(b, h, pair):
-            if (b, h) not in yT_bf:
-                yT_bf[b, h] = softmax.tile([P, TB, P], BF16, name="yT_bf")
+        def weigh(b, h, queries, pair):
+            yT_bf[b, h, pair] = softmax.tile([P, 2, P], BF16, name="yT_bf", bufs=8)
             yT_ps = summed.tile([P, 2, T // 2], F32, name="yT_ps")
-            for half in range(2):
-                jb = 2 * pair + half
+            for i in range(2):
+                jb = 2 * pair + i
                 for ib in range(jb + 1):
+                    column = e_begin[b, h, queries, ib] + jb * P - max(ib * P, queries[0])
                     nc.tensor.matmul(
-                        yT_ps[:, half, : P + 1],
-                        e_bf[b, h][:, ib, (jb - ib) * P : (jb - ib + 1) * P],
+                        yT_ps[:, i, : P + 1],
+                        e_bf[b, h, queries][:, column : column + P],
                         vT_bf[b][:, ib, h, : P + 1],
                         start=ib == 0,
                         stop=ib == jb,
                     )
-            inv_sum = softmax.tile([P, 2, 1], F32, name="inv_sum")
+            inv_sum = softmax.tile([P, 2, 1], F32, name="inv_sum", bufs=8)
             nc.vector.reciprocal(inv_sum[:], yT_ps[:, :, P : P + 1])
-            nc.vector.tensor_tensor(
-                yT_bf[b, h][:, 2 * pair : 2 * pair + 2, :], yT_ps[:, :, :P], inv_sum[:].to_broadcast([P, 2, P]), ALU.mult
-            )
+            nc.vector.tensor_tensor(yT_bf[b, h, pair][:], yT_ps[:, :, :P], inv_sum[:].to_broadcast([P, 2, P]), ALU.mult)
 
-        def turn_back(b, h):
-            y_ps = flip.tile([P, T], BF16, name="y_ps")
-            for jb in range(TB):
-                nc.tensor.transpose(y_ps[:, jb * P : (jb + 1) * P], yT_bf[b, h][:, jb, :], ident[:])
-            nc.scalar.copy(y_bf[b][:, h, :], y_ps[:])
+        def turn_back(two):
+            y_ps = flip.tile([P, 2, T // 2], BF16, name="y_ps")
+            for i, (b, h, pair) in enumerate(two):
+                for j in range(2):
+                    nc.tensor.transpose(y_ps[:, i, j * P : (j + 1) * P], yT_bf[b, h, pair][:, j, :], ident[:])
+            b, h, pair = two[0]
+            y = y_bf[b][:, h, :, :] if two[1][1] == h else y_bf[b][:, h : h + 2, pair, :]
+            nc.scalar.copy(y, y_ps[:])
 
         def add_blocks(blocks):
             partial = tail.tile([P, T], F32, name="partial")
             nc.gpsimd.tensor_tensor(partial[:], blocks[0], blocks[1], ALU.add)
             nc.gpsimd.tensor_tensor(partial[:], partial[:], blocks[2], ALU.add)
             partial_bf = tail.tile([P, T], BF16, name="partial_bf")
-            nc.vector.tensor_tensor(partial_bf[:], partial[:], blocks[3], ALU.add)
+            nc.gpsimd.tensor_tensor(partial_bf[:], partial[:], blocks[3], ALU.add)
             return partial_bf
 
         def average(partial_bf, name):
@@ -239,7 +261,9 @@ def tile_captioningtransformer_b_kernel(tc, emb, pe, wq, bq, wk, wv, bv, wo, bo,
                 nc.vector.tensor_scalar_mul(wo_shift[:, cb : cb + 1], wo_shift[:, cb : cb + 1], -1.0 / C)
                 nc.vector.tensor_scalar_add(wo_sb[:, cb, :], wo_sb[:, cb, :], wo_shift[:, cb : cb + 1])
 
-        x_sum, centred, squares, square_sum, inv_std = {}, {}, {}, {}, {}
+        whole = [(b, 0, T) for b in range(B - 1)]
+        x_sum = {}
+        centred, squares, square_sum, inv_std = {}, {}, {}, {}
 
         def centre_x(b):
             entries = slice(b * T, (b + 1) * T)
@@ -249,96 +273,125 @@ def tile_captioningtransformer_b_kernel(tc, emb, pe, wq, bq, wk, wv, bv, wo, bo,
             for cb in range(CB):
                 nc.gpsimd.tensor_tensor(x[cb][:, entries], x[cb][:, entries], mean[:], ALU.subtract)
 
-        def output_block(b, mb):
-            if b not in centred:
-                centred[b] = norm.tile([P, CB, T], F32, name="centred")
-                squares[b] = tail.tile([P, CB, T], BF16 if b == B - 1 else F32, name="squares")
+        def columns(piece):
+            b, first, last = piece
+            return slice(b * T + first, b * T + last)
+
+        def output_block(piece, mb):
+            b, first, last = piece
+            if piece not in centred:
+                centred[piece] = (norm if b < B - 1 else ending).tile([P, CB, last - first], F32, name="centred")
+                squares[piece] = squared.tile([P, CB, last - first], F32 if piece in whole[:2] else BF16, name="squares")
             z_ps = acc.tile([P, T], F32, name="z_ps", tag="acc")
+            y = y_bf[b][:].rearrange("p h half position -> p h (half position)")
             for cb in range(CB):
                 nc.tensor.matmul(
-                    z_ps[:], wo_sb[:, cb, mb * P : (mb + 1) * P], y_bf[b][:, cb, :], start=cb == 0, stop=cb == CB - 1
+                    z_ps[:, : last - first],
+                    wo_sb[:, cb, mb * P : (mb + 1) * P],
+                    y[:, cb, first:last],
+                    start=cb == 0,
+                    stop=cb == CB - 1,
                 )
             nc.vector.scalar_tensor_tensor(
-                centred[b][:, mb, :], z_ps[:], vectors[:, mb, BO : BO + 1], x[mb][:, b * T : (b + 1) * T], ALU.add, ALU.add
+                centred[piece][:, mb, :],
+                z_ps[:, : last - first],
+                vectors[:, mb, BO : BO + 1],
+                x[mb][:, columns(piece)],
+                ALU.add,
+                ALU.add,
             )
-            nc.scalar.square(squares[b][:, mb, :], centred[b][:, mb, :])
+            nc.scalar.square(squares[piece][:, mb, :], centred[piece][:, mb, :])
 
-        def normalise_block(b, mb):
-            normed = leaving.tile([P, T], F32, name="normed")
-            nc.vector.tensor_tensor(normed[:], centred[b][:, mb, :], inv_std[b][:], ALU.mult)
-            result = stored.tile([P, T], F32, name="result")
-            nc.scalar.activation(
-                result[:],
-                normed[:],
-                FUNC.Identity,
-                bias=vectors[:, mb, LN_B : LN_B + 1],
-                scale=vectors[:, mb, LN_W : LN_W + 1],
-            )
-            nc.sync.dma_start(out[mb * P : (mb + 1) * P, b * T : (b + 1) * T], result[:])
-
-        def store_deviation(b, var_ps):
-            inv_std[b] = tail.tile([P, T], F32, name="inv_std")
-            nc.scalar.activation(inv_std[b][:], var_ps[:], FUNC.Abs_reciprocal_sqrt, bias=eps[:])
-
-        def deviation(b, pool, tag):
+        def deviation(piece, pool, tag):
+            b, first, last = piece
+            blocks = [square_sum[piece][:]] if piece in square_sum else [squares[piece][:, i, :] for i in range(CB)]
             var_ps = pool.tile([P, T], F32, name="var_ps", tag=tag)
-            nc.tensor.matmul(var_ps[:], averager[:], square_sum[b][:], start=True, stop=True)
-            store_deviation(b, var_ps)
+            for i, block in enumerate(blocks):
+                nc.tensor.matmul(var_ps[:, : last - first], averager[:], block, start=i == 0, stop=i == len(blocks) - 1)
+            inv_std[piece] = (tail if b < B - 1 else ending).tile([P, last - first], F32, name="inv_std")
+            nc.scalar.activation(inv_std[piece][:], var_ps[:, : last - first], FUNC.Abs_reciprocal_sqrt, bias=eps[:])
+
+        def normalise_block(piece, mb):
+            b, first, last = piece
+            normed = leaving.tile([P, last - first], F32, name="normed")
+            result = stored.tile([P, last - first], F32, name="result")
+            weight, bias = vectors[:, mb, LN_W : LN_W + 1], vectors[:, mb, LN_B : LN_B + 1]
+            if b == 1:
+                nc.gpsimd.tensor_tensor(normed[:], centred[piece][:, mb, :], inv_std[piece][:], ALU.mult)
+                nc.gpsimd.tensor_scalar(result[:], normed[:], weight, bias, ALU.mult, ALU.add)
+            else:
+                nc.vector.tensor_tensor(normed[:], centred[piece][:, mb, :], inv_std[piece][:], ALU.mult)
+                nc.scalar.activation(result[:], normed[:], FUNC.Identity, bias=bias, scale=weight)
+            nc.sync.dma_start(out[mb * P : (mb + 1) * P, columns(piece)], result[:])
 
         P_LEAD = 2
-        Z_LAG = H + 2
-        N_LAG = Z_LAG + CB
         STEPS = B * H
+        Z_STEPS = (H + 2, 2 * H + 2, STEPS + 1)
+        N_STEP = Z_STEPS[0] + 5
+        all_queries, halves = (0, T), ((0, T // 2), (T // 2, T))
+        items = [(b, h, all_queries, (pair,), pair) for b in range(B - 1) for h in range(H) for pair in range(2)]
+        items += [(B - 1, h, halves[pair], tuple(range(pair + 1)), pair) for pair in range(2) for h in range(H)]
+        half_0, half_1 = (B - 1, 0, T // 2), (B - 1, T // 2, T)
         for h in range(P_LEAD):
             project_k(0, h)
         for ib in range(P_LEAD):
             project_v(0, ib)
         for step in range(STEPS + 3):
-            b, h = divmod(step, H)
             pb, ph = divmod(step + P_LEAD, H)
-            zb, z_mb = divmod(step - Z_LAG, CB)
-            nb, n_mb = divmod(step - N_LAG, CB)
+            scored, weighed, turned = (items[2 * s : 2 * s + 2] if 0 <= s < STEPS else [] for s in (step, step - 2, step - 3))
             if ph == 0 and 1 <= pb < B:
                 new_caption(pb)
-            if b < B:
-                scores(b, h, (0, 1))
+            if scored:
+                scores(*scored[0][:4])
             if 1 <= pb < B:
                 project_q(pb, ph)
-            if 3 <= step:
-                turn_back((step - 3) // H, (step - 3) % H)
+            if turned:
+                turn_back([(b, h, pair) for b, h, queries, key_pairs, pair in turned])
             if pb < B:
                 project_k(pb, ph)
-            if b < B:
-                scores(b, h, (2, 3))
-            if nb >= 0 and n_mb == 0 and b + 1 < B:
-                deviation(nb, acc, "acc")
-            if 2 <= step <= STEPS + 1:
-                weigh((step - 2) // H, (step - 2) % H, 0)
+            if scored:
+                scores(*scored[1][:4])
+            if step == N_STEP:
+                deviation(whole[0], acc, "acc")
+            if step == STEPS:
+                deviation(whole[1], score, "s_ps")
+            if weighed:
+                weigh(*weighed[0][:3], weighed[0][4])
             if pb < B:
                 project_v(pb, ph)
-            if 2 <= step <= STEPS + 1:
-                weigh((step - 2) // H, (step - 2) % H, 1)
-            if step == Z_LAG - 1:
+            if weighed:
+                weigh(*weighed[1][:3], weighed[1][4])
+            if step == Z_STEPS[0] - 1:
                 centre_wo()
-            if h == 2 and b < B:
-                x_sum[b] = add_blocks([x[cb][:, b * T : (b + 1) * T] for cb in range(CB)])
-            if h == 3 and b < B:
-                centre_x(b)
-            if 0 <= zb < B - 1:
-                output_block(zb, z_mb)
-                if z_mb == CB - 1:
-                    square_sum[zb] = add_blocks([squares[zb][:, i, :] for i in range(CB)])
-            if nb in inv_std:
-                normalise_block(nb, n_mb)
+            cx, later = divmod(step - 2, 2)
+            if 0 <= cx < B:
+                if later:
+                    centre_x(cx)
+                else:
+                    x_sum[cx] = add_blocks([x[cb][:, cx * T : (cx + 1) * T] for cb in range(CB)])
+            for piece, z_step in zip(whole, Z_STEPS):
+                if step == z_step:
+                    output_block(piece, 0)
+                    output_block(piece, 1)
+                if step == z_step + 1:
+                    output_block(piece, 2)
+                    output_block(piece, 3)
+                    if piece in whole[:2]:
+                        square_sum[piece] = add_blocks([squares[piece][:, i, :] for i in range(CB)])
+            if N_STEP <= step < N_STEP + CB:
+                normalise_block(whole[0], step - N_STEP)
+            if step == STEPS:
+                for mb in range(CB):
+                    normalise_block(whole[1], mb)
 
-        waiting = [nb for nb in range(B - 1) if nb not in inv_std]
-        for nb in waiting:
-            deviation(nb, score, "s_ps")
-        var_ps = summed.tile([P, T], F32, name="var_ps", tag="yT_ps")
         for mb in range(CB):
-            output_block(B - 1, mb)
-            nc.tensor.matmul(var_ps[:], averager[:], squares[B - 1][:, mb, :], start=mb == 0, stop=mb == CB - 1)
-        store_deviation(B - 1, var_ps)
-        for nb in waiting + [B - 1]:
+            output_block(half_0, mb)
+        waiting = [whole[2], half_0]
+        for piece in waiting:
+            deviation(piece, score, "s_ps")
+        for mb in range(CB):
+            output_block(half_1, mb)
+        deviation(half_1, acc, "acc")
+        for piece in waiting + [half_1]:
             for mb in range(CB):
-                normalise_block(nb, mb)
+                normalise_block(piece, mb)

@@ -72,18 +72,13 @@ def tile_captioningtransformer_b_kernel(tc, emb, pe, wq, bq, wk, wv, bv, wo, bo,
             wo_sb = held.tile([P, CB, C], BF16, name="wo_sb")
             nc.sync.dma_start(wo_sb[:], wo.rearrange("(cb p) m -> p cb m", p=P))
 
-            bo_shift = start.tile([1, 1], F32, name="bo_shift")
-            nc.vector.reduce_sum(bo_shift[:], rows[BO : BO + 1, :], axis=mybir.AxisListType.X)
-            nc.vector.tensor_scalar_mul(bo_shift[:], bo_shift[:], -1.0 / C)
-            nc.vector.tensor_scalar_add(rows[BO : BO + 1, :], rows[BO : BO + 1, :], bo_shift[:])
-
             ident_f32 = start.tile([ROWS, ROWS], F32, name="ident_f32")
             make_identity(nc, ident_f32[:])
             vectors = held.tile([P, CB, 4], F32, name="vectors")
             vectors_ps = flip.tile([P, CB, ROWS], F32, name="vectors_ps", tag="y_ps")
             for cb in range(CB):
                 nc.tensor.transpose(vectors_ps[:, cb, :], rows[:, cb * P : (cb + 1) * P], ident_f32[:])
-            nc.vector.tensor_copy(vectors[:], vectors_ps[:, :, 0:4])
+            nc.scalar.copy(vectors[:], vectors_ps[:, :, 0:4])
 
             ident = held.tile([P, P], BF16, name="ident")
             make_identity(nc, ident[:])
@@ -125,8 +120,8 @@ def tile_captioningtransformer_b_kernel(tc, emb, pe, wq, bq, wk, wv, bv, wo, bo,
                 q_early[b] = norm.tile([P, H, T], F32, name="q_early", tag="centred")
                 for h in range(H):
                     early_ps = acc.tile([P, T], F32, name="early_ps", tag="acc")
-                    add_to_q(early_ps, b, h, range(b + 1))
-                    nc.scalar.activation(q_early[b][:, h, :], early_ps[:], FUNC.Identity, bias=vectors[:, h, BQ : BQ + 1])
+                    add_to_q(early_ps, b, h, range(B - b))
+                    nc.scalar.copy(q_early[b][:, h, :], early_ps[:])
 
             new_caption(0)
             q_ps = [score.tile([P, T], F32, name=f"q_ps{h}", tag="s_ps") for h in range(2)]
@@ -140,9 +135,10 @@ def tile_captioningtransformer_b_kernel(tc, emb, pe, wq, bq, wk, wv, bv, wo, bo,
                 if cb == CB - 1:
                     for h in range(H):
                         nc.scalar.activation(q_bf[0][:, h, :], q_ps[h][:], FUNC.Identity, bias=vectors[:, h, BQ : BQ + 1])
-                if cb >= 2:
-                    sum_early(cb - 1)
-                for b in range(1, B):
+                if cb > 0:
+                    sum_early(B - cb)
+                early = B - 1 - cb
+                for b in [early] * (early > 0) + [b for b in range(1, B) if b != early]:
                     look_up(cb, b)
 
         tail = ctx.enter_context(tc.tile_pool(name="tail", bufs=3))
@@ -153,12 +149,10 @@ def tile_captioningtransformer_b_kernel(tc, emb, pe, wq, bq, wk, wv, bv, wo, bo,
 
         def project_q(b, h):
             q_ps = acc.tile([P, T], F32, name="q_ps", tag="acc")
-            if b in q_early:
-                add_to_q(q_ps, b, h, range(b + 1, CB))
-                nc.vector.tensor_tensor(q_bf[b][:, h, :], q_ps[:], q_early[b][:, h, :], ALU.add)
-            else:
-                add_to_q(q_ps, b, h, range(CB))
-                nc.scalar.activation(q_bf[b][:, h, :], q_ps[:], FUNC.Identity, bias=vectors[:, h, BQ : BQ + 1])
+            add_to_q(q_ps, b, h, range(B - b, CB))
+            nc.vector.scalar_tensor_tensor(
+                q_bf[b][:, h, :], q_ps[:], vectors[:, h, BQ : BQ + 1], q_early[b][:, h, :], ALU.add, ALU.add
+            )
 
         def project_k(b, h):
             k_ps = acc.tile([P, T], F32, name="k_ps", tag="acc")
@@ -255,6 +249,14 @@ def tile_captioningtransformer_b_kernel(tc, emb, pe, wq, bq, wk, wv, bv, wo, bo,
             return mean_ps
 
         def centre_wo():
+            bo_bf = held.tile([P, CB], BF16, name="bo_bf")
+            nc.vector.tensor_copy(bo_bf[:], vectors[:, :, BO])
+            mean_ps = acc.tile([P, T], F32, name="mean_ps", tag="acc")
+            for cb in range(CB):
+                nc.tensor.matmul(mean_ps[:, 0:1], averager[:], bo_bf[:, cb : cb + 1], start=cb == 0, stop=cb == CB - 1)
+            bo_mean = held.tile([P, 1], F32, name="bo_mean")
+            nc.vector.tensor_copy(bo_mean[:], mean_ps[:, 0:1])
+            nc.vector.tensor_scalar_sub(vectors[:, :, BO], vectors[:, :, BO], bo_mean[:])
             wo_shift = held.tile([P, CB], F32, name="wo_shift")
             for cb in range(CB):
                 nc.vector.reduce_sum(wo_shift[:, cb : cb + 1], wo_sb[:, cb, :], axis=mybir.AxisListType.X)

@@ -318,12 +318,8 @@ def tile_captioningtransformer_b_kernel(tc, emb, pe, wq, bq, wk, wv, bv, wo, bo,
             normed = leaving.tile([P, last - first], F32, name="normed")
             result = stored.tile([P, last - first], F32, name="result")
             weight, bias = vectors[:, mb, LN_W : LN_W + 1], vectors[:, mb, LN_B : LN_B + 1]
-            if b == 1:
-                nc.gpsimd.tensor_tensor(normed[:], centred[piece][:, mb, :], inv_std[piece][:], ALU.mult)
-                nc.gpsimd.tensor_scalar(result[:], normed[:], weight, bias, ALU.mult, ALU.add)
-            else:
-                nc.vector.tensor_tensor(normed[:], centred[piece][:, mb, :], inv_std[piece][:], ALU.mult)
-                nc.scalar.activation(result[:], normed[:], FUNC.Identity, bias=bias, scale=weight)
+            nc.vector.tensor_tensor(normed[:], centred[piece][:, mb, :], inv_std[piece][:], ALU.mult)
+            nc.scalar.activation(result[:], normed[:], FUNC.Identity, bias=bias, scale=weight)
             nc.sync.dma_start(out[mb * P : (mb + 1) * P, columns(piece)], result[:])
 
         P_LEAD = 2

@@ -160,7 +160,10 @@ def tile_captioningtransformer_b_kernel(tc, emb, pe, wq, bq, wk, wv, bv, wo, bo,
                 nc.tensor.matmul(
                     k_ps[:], wk_sb[:, cb, h * P : (h + 1) * P], x_bf[cb][:, b * T : (b + 1) * T], start=cb == 0, stop=cb == CB - 1
                 )
-            nc.vector.tensor_copy(k_bf[b][:, h, :], k_ps[:])
+            if b == 0:
+                nc.vector.tensor_copy(k_bf[b][:, h, :], k_ps[:])
+            else:
+                nc.scalar.copy(k_bf[b][:, h, :], k_ps[:])
 
         def project_v(b, ib):
             keys = slice(b * T + ib * P, b * T + (ib + 1) * P)
@@ -319,7 +322,10 @@ def tile_captioningtransformer_b_kernel(tc, emb, pe, wq, bq, wk, wv, bv, wo, bo,
             result = stored.tile([P, last - first], F32, name="result")
             weight, bias = vectors[:, mb, LN_W : LN_W + 1], vectors[:, mb, LN_B : LN_B + 1]
             nc.vector.tensor_tensor(normed[:], centred[piece][:, mb, :], inv_std[piece][:], ALU.mult)
-            nc.scalar.activation(result[:], normed[:], FUNC.Identity, bias=bias, scale=weight)
+            if b == B - 1:
+                nc.vector.tensor_scalar(result[:], normed[:], weight, bias, ALU.mult, ALU.add)
+            else:
+                nc.scalar.activation(result[:], normed[:], FUNC.Identity, bias=bias, scale=weight)
             nc.sync.dma_start(out[mb * P : (mb + 1) * P, columns(piece)], result[:])
 
         P_LEAD = 2
@@ -378,18 +384,19 @@ def tile_captioningtransformer_b_kernel(tc, emb, pe, wq, bq, wk, wv, bv, wo, bo,
                         square_sum[piece] = add_blocks([squares[piece][:, i, :] for i in range(CB)])
             if N_STEP <= step < N_STEP + CB:
                 normalise_block(whole[0], step - N_STEP)
-            if step == STEPS:
-                for mb in range(CB):
-                    normalise_block(whole[1], mb)
 
+        deviation(whole[2], score, "s_ps")
         for mb in range(CB):
             output_block(half_0, mb)
-        waiting = [whole[2], half_0]
-        for piece in waiting:
-            deviation(piece, score, "s_ps")
+        deviation(half_0, score, "s_ps")
         for mb in range(CB):
             output_block(half_1, mb)
         deviation(half_1, acc, "acc")
-        for piece in waiting + [half_1]:
-            for mb in range(CB):
-                normalise_block(piece, mb)
+        for mb in range(CB):
+            normalise_block(whole[1], mb)
+        for mb in range(CB):
+            normalise_block(whole[2], mb)
+        for mb in range(CB):
+            normalise_block(half_0, mb)
+        for mb in range(CB):
+            normalise_block(half_1, mb)

@@ -28,7 +28,7 @@ def tile_captioningtransformer_b_kernel(tc, emb, pe, wq, bq, wk, wv, bv, wo, bo,
     with ExitStack() as ctx:
         held = ctx.enter_context(tc.tile_pool(name="held", bufs=1))
         caption = ctx.enter_context(tc.tile_pool(name="caption", bufs=3))
-        softmax = ctx.enter_context(tc.tile_pool(name="softmax", bufs=6))
+        softmax = ctx.enter_context(tc.tile_pool(name="softmax", bufs=8))
 
         offsets = held.tile([P, N // 16], U16, name="offsets")
         nc.sync.dma_start(offsets[:], offs)
@@ -38,8 +38,8 @@ def tile_captioningtransformer_b_kernel(tc, emb, pe, wq, bq, wk, wv, bv, wo, bo,
         q_early, q_bf, k_bf, vT_bf, y_bf = {}, {}, {}, {}, {}
 
         def new_caption(b):
-            q_bf[b] = caption.tile([P, H, T], BF16, name="q_bf")
-            k_bf[b] = caption.tile([P, H, T], BF16, name="k_bf")
+            q_bf[b] = caption.tile([P, H, T], BF16, name="q_bf", bufs=2)
+            k_bf[b] = caption.tile([P, H, T], BF16, name="k_bf", bufs=2)
             vT_bf[b] = caption.tile([P, TB, H, VW], BF16, name="vT_bf")
             nc.gpsimd.memset(vT_bf[b][:, :, :, P : P + 1], 1.0)
             y_bf[b] = caption.tile([P, H, 2, T // 2], BF16, name="y_bf")
@@ -330,7 +330,7 @@ def tile_captioningtransformer_b_kernel(tc, emb, pe, wq, bq, wk, wv, bv, wo, bo,
 
         P_LEAD = 2
         STEPS = B * H
-        Z_STEPS = (H + 2, 2 * H + 2, STEPS + 1)
+        Z_STEPS = (H + 3, 2 * H + 3, STEPS + 2)
         N_STEP = Z_STEPS[0] + 5
         all_queries, halves = (0, T), ((0, T // 2), (T // 2, T))
         items = [(b, h, all_queries, (pair,), pair) for b in range(B - 1) for h in range(H) for pair in range(2)]
@@ -340,9 +340,9 @@ def tile_captioningtransformer_b_kernel(tc, emb, pe, wq, bq, wk, wv, bv, wo, bo,
             project_k(0, h)
         for ib in range(P_LEAD):
             project_v(0, ib)
-        for step in range(STEPS + 3):
+        for step in range(STEPS + 4):
             pb, ph = divmod(step + P_LEAD, H)
-            scored, weighed, turned = (items[2 * s : 2 * s + 2] if 0 <= s < STEPS else [] for s in (step, step - 2, step - 3))
+            scored, weighed, turned = (items[2 * s : 2 * s + 2] if 0 <= s < STEPS else [] for s in (step, step - 3, step - 4))
             if ph == 0 and 1 <= pb < B:
                 new_caption(pb)
             if scored:

@@ -154,28 +154,26 @@ def tile_captioningtransformer_b_kernel(tc, emb, pe, wq, bq, wk, wv, bv, wo, bo,
                 q_bf[b][:, h, :], q_ps[:], vectors[:, h, BQ : BQ + 1], q_early[b][:, h, :], ALU.add, ALU.add
             )
 
+        def leave_psum(b, kept, sums):
+            if b == 0:
+                nc.vector.tensor_copy(kept, sums)
+            else:
+                nc.scalar.copy(kept, sums)
+
         def project_k(b, h):
             k_ps = acc.tile([P, T], F32, name="k_ps", tag="acc")
             for cb in range(CB):
                 nc.tensor.matmul(
                     k_ps[:], wk_sb[:, cb, h * P : (h + 1) * P], x_bf[cb][:, b * T : (b + 1) * T], start=cb == 0, stop=cb == CB - 1
                 )
-            if b == 0:
-                nc.vector.tensor_copy(k_bf[b][:, h, :], k_ps[:])
-            else:
-                nc.scalar.copy(k_bf[b][:, h, :], k_ps[:])
+            leave_psum(b, k_bf[b][:, h, :], k_ps[:])
 
         def project_v(b, ib):
             keys = slice(b * T + ib * P, b * T + (ib + 1) * P)
             v_ps = acc.tile([P, C], F32, name="v_ps", tag="acc")
             for cb in range(CB):
                 nc.tensor.matmul(v_ps[:], x_bf[cb][:, keys], wv_sb[:, cb, :], start=cb == 0, stop=cb == CB - 1)
-            nc.vector.tensor_tensor(
-                vT_bf[b][:, ib, :, :P],
-                v_ps[:].rearrange("p (h d) -> p h d", h=H),
-                bv_rows[:].rearrange("p (h d) -> p h d", h=H),
-                ALU.add,
-            )
+            leave_psum(b, vT_bf[b][:, ib, :, :P], v_ps[:].rearrange("p (h d) -> p h d", h=H))
 
         e_bf, e_begin, yT_bf = {}, {}, {}
 
@@ -227,7 +225,10 @@ def tile_captioningtransformer_b_kernel(tc, emb, pe, wq, bq, wk, wv, bv, wo, bo,
                     )
             inv_sum = softmax.tile([P, 2, 1], F32, name="inv_sum", bufs=8)
             nc.vector.reciprocal(inv_sum[:], yT_ps[:, :, P : P + 1])
-            nc.vector.tensor_tensor(yT_bf[b, h, pair][:], yT_ps[:, :, :P], inv_sum[:].to_broadcast([P, 2, P]), ALU.mult)
+            for i in range(2):
+                nc.vector.scalar_tensor_tensor(
+                    yT_bf[b, h, pair][:, i, :], yT_ps[:, i, :P], inv_sum[:, i, :], bv_rows[:, h * P : (h + 1) * P], ALU.mult, ALU.add
+                )
 
         def turn_back(two):
             y_ps = flip.tile([P, 2, T // 2], BF16, name="y_ps")

@@ -28,7 +28,7 @@ def tile_captioningtransformer_b_kernel(tc, emb, pe, wq, bq, wk, wv, bv, wo, bo,
     with ExitStack() as ctx:
         held = ctx.enter_context(tc.tile_pool(name="held", bufs=1))
         caption = ctx.enter_context(tc.tile_pool(name="caption", bufs=3))
-        softmax = ctx.enter_context(tc.tile_pool(name="softmax", bufs=8))
+        softmax = ctx.enter_context(tc.tile_pool(name="softmax", bufs=10))
 
         offsets = held.tile([P, N // 16], U16, name="offsets")
         nc.sync.dma_start(offsets[:], offs)
@@ -210,7 +210,7 @@ def tile_captioningtransformer_b_kernel(tc, emb, pe, wq, bq, wk, wv, bv, wo, bo,
                     nc.vector.tensor_tensor(diagonal, diagonal, mask[:].to_broadcast([P, 2, P]), ALU.mult)
 
         def weigh(b, h, queries, pair):
-            yT_bf[b, h, pair] = softmax.tile([P, 2, P], BF16, name="yT_bf", bufs=8)
+            yT_bf[b, h, pair] = softmax.tile([P, 2, P], BF16, name="yT_bf", bufs=6)
             yT_ps = summed.tile([P, 2, T // 2], F32, name="yT_ps")
             for i in range(2):
                 jb = 2 * pair + i
@@ -331,7 +331,7 @@ def tile_captioningtransformer_b_kernel(tc, emb, pe, wq, bq, wk, wv, bv, wo, bo,
 
         P_LEAD = 2
         STEPS = B * H
-        Z_STEPS = (H + 3, 2 * H + 3, STEPS + 2)
+        Z_STEPS = (H + 4, 2 * H + 4, STEPS + 3)
         N_STEP = Z_STEPS[0] + 5
         all_queries, halves = (0, T), ((0, T // 2), (T // 2, T))
         items = [(b, h, all_queries, (pair,), pair) for b in range(B - 1) for h in range(H) for pair in range(2)]
@@ -341,9 +341,9 @@ def tile_captioningtransformer_b_kernel(tc, emb, pe, wq, bq, wk, wv, bv, wo, bo,
             project_k(0, h)
         for ib in range(P_LEAD):
             project_v(0, ib)
-        for step in range(STEPS + 4):
+        for step in range(STEPS + 5):
             pb, ph = divmod(step + P_LEAD, H)
-            scored, weighed, turned = (items[2 * s : 2 * s + 2] if 0 <= s < STEPS else [] for s in (step, step - 3, step - 4))
+            scored, weighed, turned = (items[2 * s : 2 * s + 2] if 0 <= s < STEPS else [] for s in (step, step - 4, step - 5))
             if ph == 0 and 1 <= pb < B:
                 new_caption(pb)
             if scored:

import math
from contextlib import ExitStack

import concourse.mybir as mybir
from concourse.masks import make_identity

F32 = mybir.dt.float32
BF16 = mybir.dt.bfloat16
U16 = mybir.dt.uint16
ALU = mybir.AluOpType
FUNC = mybir.ActivationFunctionType

P = 128
C, S, N, B, T, H = 512, 4096, 2048, 4, 512, 4
CB = C // P
TB = T // P
EPS = 1e-5
INV_SQRT_DH = 1.0 / math.sqrt(P)
VW = 144
ROWS = 64
BO, BQ, LN_W, LN_B = 0, 1, 2, 3

FLOPS = 4 * 2 * C * C * N + 2 * 2 * P * (T * (T + 1) // 2) * B * H


def tile_captioningtransformer_b_kernel(tc, emb, pe, wq, bq, wk, wv, bv, wo, bo, ln_w, ln_b, offs, out):
    nc = tc.nc
    with ExitStack() as ctx:
        held = ctx.enter_context(tc.tile_pool(name="held", bufs=1))
        caption = ctx.enter_context(tc.tile_pool(name="caption", bufs=3))
        softmax = ctx.enter_context(tc.tile_pool(name="softmax", bufs=10))

        offsets = held.tile([P, N // 16], U16, name="offsets")
        nc.sync.dma_start(offsets[:], offs)

        x = [held.tile([P, N], F32, name=f"x{cb}") for cb in range(CB)]
        x_bf = [held.tile([P, N], BF16, name=f"x_bf{cb}") for cb in range(CB)]
        q_early, q_bf, k_bf, vT_bf, y_bf = {}, {}, {}, {}, {}

        def new_caption(b):
            q_bf[b] = caption.tile([P, H, T], BF16, name="q_bf", bufs=2)
            k_bf[b] = caption.tile([P, H, T], BF16, name="k_bf", bufs=2)
            vT_bf[b] = caption.tile([P, TB, H, VW], BF16, name="vT_bf")
            nc.gpsimd.memset(vT_bf[b][:, :, :, P : P + 1], 1.0)
            y_bf[b] = caption.tile([P, H, 2, T // 2], BF16, name="y_bf")

        norm = ctx.enter_context(tc.tile_pool(name="norm", bufs=3))
        acc = ctx.enter_context(tc.psum_pool(name="acc", bufs=3))
        score = ctx.enter_context(tc.psum_pool(name="score", bufs=2))
        summed = ctx.enter_context(tc.psum_pool(name="summed", bufs=2))
        flip = ctx.enter_context(tc.psum_pool(name="flip", bufs=1))

        with tc.tile_pool(name="start", bufs=1) as start:
            rows = start.tile([ROWS, C], F32, name="rows")
            nc.vector.memset(rows[:], 0.0)
            pos = [start.tile([P, T], F32, name=f"pos{cb}") for cb in range(CB)]
            table = [start.tile([P, S], F32, name=f"table{cb}") for cb in range(CB)]
            wq_sb = held.tile([P, CB, C], BF16, name="wq_sb")
            for cb in range(CB):
                nc.sync.dma_start(pos[cb][:], pe[cb * P : (cb + 1) * P, :])
                nc.sync.dma_start(table[cb][:], emb[cb * P : (cb + 1) * P, :])
                if cb == 0:
                    nc.sync.dma_start(wq_sb[:], wq.rearrange("(cb p) m -> p cb m", p=P))
                    for r, vector in ((BO, bo), (BQ, bq), (LN_W, ln_w), (LN_B, ln_b)):
                        nc.sync.dma_start(rows[r : r + 1, :], vector.rearrange("c one -> one c"))
            wk_sb = held.tile([P, CB, C], BF16, name="wk_sb")
            nc.sync.dma_start(wk_sb[:], wk.rearrange("(cb p) m -> p cb m", p=P))
            wv_sb = held.tile([P, CB, C], BF16, name="wv_sb")
            nc.sync.dma_start(wv_sb[:], wv.rearrange("(cb p) m -> p cb m", p=P))
            bv_rows = held.tile([P, C], F32, name="bv_rows")
            nc.sync.dma_start(bv_rows[:], bv.rearrange("c one -> (c one)").partition_broadcast(P))
            wo_sb = held.tile([P, CB, C], BF16, name="wo_sb")
            nc.sync.dma_start(wo_sb[:], wo.rearrange("(cb p) m -> p cb m", p=P))

            ident_f32 = start.tile([ROWS, ROWS], F32, name="ident_f32")
            make_identity(nc, ident_f32[:])
            vectors = held.tile([P, CB, 4], F32, name="vectors")
            vectors_ps = flip.tile([P, CB, ROWS], F32, name="vectors_ps", tag="y_ps")
            for cb in range(CB):
                nc.tensor.transpose(vectors_ps[:, cb, :], rows[:, cb * P : (cb + 1) * P], ident_f32[:])
            nc.scalar.copy(vectors[:], vectors_ps[:, :, 0:4])

            ident = held.tile([P, P], BF16, name="ident")
            make_identity(nc, ident[:])
            mask_f32 = start.tile([P, P], F32, name="mask_f32")
            nc.gpsimd.memset(mask_f32[:], 1.0)
            nc.gpsimd.affine_select(
                out=mask_f32[:],
                in_=mask_f32[:],
                compare_op=ALU.is_ge,
                fill=0.0,
                base=0,
                pattern=[[1, P]],
                channel_multiplier=-1,
            )
            mask = held.tile([P, 1, P], BF16, name="mask")
            nc.vector.tensor_copy(mask[:, 0, :], mask_f32[:])
            averager = held.tile([P, P], BF16, name="averager")
            nc.vector.memset(averager[:], 1.0 / C)
            eps = held.tile([P, 1], F32, name="eps")
            nc.vector.memset(eps[:], EPS)

            def look_up(cb, b):
                entries = slice(b * T, (b + 1) * T)
                picked = table[cb][:].indirect(offsets[:, b * T // 16 : (b + 1) * T // 16])
                nc.vector.tensor_tensor(x[cb][:, entries], picked, pos[cb][:], ALU.add)
                nc.scalar.copy(x_bf[cb][:, entries], x[cb][:, entries])

            def add_to_q(q_ps, b, h, cbs):
                for cb in cbs:
                    nc.tensor.matmul(
                        q_ps[:],
                        wq_sb[:, cb, h * P : (h + 1) * P],
                        x_bf[cb][:, b * T : (b + 1) * T],
                        start=cb == cbs[0],
                        stop=cb == cbs[-1],
                    )

            def sum_early(b):
                q_early[b] = norm.tile([P, H, T], F32, name="q_early", tag="centred")
                for h in range(H):
                    early_ps = acc.tile([P, T], F32, name="early_ps", tag="acc")
                    add_to_q(early_ps, b, h, range(B - b))
                    nc.scalar.copy(q_early[b][:, h, :], early_ps[:])

            new_caption(0)
            q_ps = [score.tile([P, T], F32, name=f"q_ps{h}", tag="s_ps") for h in range(2)]
            q_ps += [summed.tile([P, T], F32, name=f"q_ps{h}", tag="yT_ps") for h in range(2, 4)]
            for cb in range(CB):
                look_up(cb, 0)
                for h in range(H):
                    nc.tensor.matmul(
                        q_ps[h][:], wq_sb[:, cb, h * P : (h + 1) * P], x_bf[cb][:, :T], start=cb == 0, stop=cb == CB - 1
                    )
                if cb == CB - 1:
                    for h in range(H):
                        nc.scalar.activation(q_bf[0][:, h, :], q_ps[h][:], FUNC.Identity, bias=vectors[:, h, BQ : BQ + 1])
                if cb > 0:
                    sum_early(B - cb)
                early = B - 1 - cb
                for b in [early] * (early > 0) + [b for b in range(1, B) if b != early]:
                    look_up(cb, b)

        tail = ctx.enter_context(tc.tile_pool(name="tail", bufs=3))
        squared = ctx.enter_context(tc.tile_pool(name="squared", bufs=2))
        ending = ctx.enter_context(tc.tile_pool(name="ending", bufs=2))
        leaving = ctx.enter_context(tc.tile_pool(name="leaving", bufs=4))
        stored = ctx.enter_context(tc.tile_pool(name="stored", bufs=8))

        def project_q(b, h):
            q_ps = acc.tile([P, T], F32, name="q_ps", tag="acc")
            add_to_q(q_ps, b, h, range(B - b, CB))
            nc.vector.scalar_tensor_tensor(
                q_bf[b][:, h, :], q_ps[:], vectors[:, h, BQ : BQ + 1], q_early[b][:, h, :], ALU.add, ALU.add
            )

        def leave_psum(b, kept, sums):
            if b == 0:
                nc.vector.tensor_copy(kept, sums)
            else:
                nc.scalar.copy(kept, sums)

        def project_k(b, h):
            k_ps = acc.tile([P, T], F32, name="k_ps", tag="acc")
            for cb in range(CB):
                nc.tensor.matmul(
                    k_ps[:], wk_sb[:, cb, h * P : (h + 1) * P], x_bf[cb][:, b * T : (b + 1) * T], start=cb == 0, stop=cb == CB - 1
                )
            leave_psum(b, k_bf[b][:, h, :], k_ps[:])

        def project_v(b, ib):
            keys = slice(b * T + ib * P, b * T + (ib + 1) * P)
            v_ps = acc.tile([P, C], F32, name="v_ps", tag="acc")
            for cb in range(CB):
                nc.tensor.matmul(v_ps[:], x_bf[cb][:, keys], wv_sb[:, cb, :], start=cb == 0, stop=cb == CB - 1)
            leave_psum(b, vT_bf[b][:, ib, :, :P], v_ps[:].rearrange("p (h d) -> p h d", h=H))

        e_bf, e_begin, yT_bf = {}, {}, {}

        def scores(b, h, queries, key_pairs):
            head = (b, h, queries)
            if head not in e_bf:
                first, last = queries
                begin = 0
                for ib in range(last // P):
                    e_begin[b, h, queries, ib] = begin
                    begin += last - max(ib * P, first)
                e_bf[head] = softmax.tile([P, begin + P], BF16, name="e_bf")
            for pair in key_pairs:
                banks = [(2 * pair, 2 * pair + 1)]
                if queries[1] - queries[0] > T // 2 and pair == 0:
                    banks = [(0,), (1,)]
                for bank in banks:
                    s_ps = score.tile([P, T], F32, name="s_ps")
                    origin = e_begin[b, h, queries, bank[0]]
                    for ib in bank:
                        seen = slice(max(ib * P, queries[0]), queries[1])
                        begin = e_begin[b, h, queries, ib] - origin
                        end = begin + seen.stop - seen.start
                        nc.tensor.matmul(
                            s_ps[:, begin:end], k_bf[b][:, h, ib * P : (ib + 1) * P], q_bf[b][:, h, seen], start=True, stop=True
                        )
                    nc.scalar.activation(
                        e_bf[head][:, origin : origin + end], s_ps[:, :end], FUNC.Exp, scale=INV_SQRT_DH
                    )
                if 2 * pair * P >= queries[0]:
                    begin = e_begin[b, h, queries, 2 * pair]
                    width = e_begin[b, h, queries, 2 * pair + 1] - begin
                    diagonal = e_bf[head][:, begin : begin + 2 * width].rearrange("p (two q) -> p two q", two=2)[:, :, :P]
                    nc.vector.tensor_tensor(diagonal, diagonal, mask[:].to_broadcast([P, 2, P]), ALU.mult)

        def weigh(b, h, queries, pair):
            yT_bf[b, h, pair] = softmax.tile([P, 2, P], BF16, name="yT_bf", bufs=6)
            yT_ps = summed.tile([P, 2, T // 2], F32, name="yT_ps")
            for i in range(2):
                jb = 2 * pair + i
                for ib in range(jb + 1):
                    column = e_begin[b, h, queries, ib] + jb * P - max(ib * P, queries[0])
                    nc.tensor.matmul(
                        yT_ps[:, i, : P + 1],
                        e_bf[b, h, queries][:, column : column + P],
                        vT_bf[b][:, ib, h, : P + 1],
                        start=ib == 0,
                        stop=ib == jb,
                    )
            inv_sum = softmax.tile([P, 2, 1], F32, name="inv_sum", bufs=8)
            nc.vector.reciprocal(inv_sum[:], yT_ps[:, :, P : P + 1])
            for i in range(2):
                nc.vector.scalar_tensor_tensor(
                    yT_bf[b, h, pair][:, i, :], yT_ps[:, i, :P], inv_sum[:, i, :], bv_rows[:, h * P : (h + 1) * P], ALU.mult, ALU.add
                )

        def turn_back(two):
            y_ps = flip.tile([P, 2, T // 2], BF16, name="y_ps")
            for i, (b, h, pair) in enumerate(two):
                for j in range(2):
                    nc.tensor.transpose(y_ps[:, i, j * P : (j + 1) * P], yT_bf[b, h, pair][:, j, :], ident[:])
            b, h, pair = two[0]
            y = y_bf[b][:, h, :, :] if two[1][1] == h else y_bf[b][:, h : h + 2, pair, :]
            nc.scalar.copy(y, y_ps[:])

        def add_blocks(blocks):
            partial = tail.tile([P, T], F32, name="partial")
            nc.gpsimd.tensor_tensor(partial[:], blocks[0], blocks[1], ALU.add)
            nc.gpsimd.tensor_tensor(partial[:], partial[:], blocks[2], ALU.add)
            partial_bf = tail.tile([P, T], BF16, name="partial_bf")
            nc.gpsimd.tensor_tensor(partial_bf[:], partial[:], blocks[3], ALU.add)
            return partial_bf

        def average(partial_bf, name):
            mean_ps = acc.tile([P, T], F32, name=name, tag="acc")
            nc.tensor.matmul(mean_ps[:], averager[:], partial_bf[:], start=True, stop=True)
            return mean_ps

        def centre_wo():
            bo_bf = held.tile([P, CB], BF16, name="bo_bf")
            nc.vector.tensor_copy(bo_bf[:], vectors[:, :, BO])
            mean_ps = acc.tile([P, T], F32, name="mean_ps", tag="acc")
            for cb in range(CB):
                nc.tensor.matmul(mean_ps[:, 0:1], averager[:], bo_bf[:, cb : cb + 1], start=cb == 0, stop=cb == CB - 1)
            bo_mean = held.tile([P, 1], F32, name="bo_mean")
            nc.vector.tensor_copy(bo_mean[:], mean_ps[:, 0:1])
            nc.vector.tensor_scalar_sub(vectors[:, :, BO], vectors[:, :, BO], bo_mean[:])
            wo_shift = held.tile([P, CB], F32, name="wo_shift")
            for cb in range(CB):
                nc.vector.reduce_sum(wo_shift[:, cb : cb + 1], wo_sb[:, cb, :], axis=mybir.AxisListType.X)
                nc.vector.tensor_scalar_mul(wo_shift[:, cb : cb + 1], wo_shift[:, cb : cb + 1], -1.0 / C)
                nc.vector.tensor_scalar_add(wo_sb[:, cb, :], wo_sb[:, cb, :], wo_shift[:, cb : cb + 1])

        whole = [(b, 0, T) for b in range(B - 1)]
        x_sum = {}
        centred, squares, square_sum, inv_std = {}, {}, {}, {}

        def centre_x(b):
            entries = slice(b * T, (b + 1) * T)
            mean_ps = average(x_sum[b], "mean_ps")
            mean = tail.tile([P, T], F32, name="mean")
            nc.scalar.copy(mean[:], mean_ps[:])
            for cb in range(CB):
                nc.gpsimd.tensor_tensor(x[cb][:, entries], x[cb][:, entries], mean[:], ALU.subtract)

        def columns(piece):
            b, first, last = piece
            return slice(b * T + first, b * T + last)

        def output_block(piece, mb):
            b, first, last = piece
            if piece not in centred:
                centred[piece] = (norm if b < B - 1 else ending).tile([P, CB, last - first], F32, name="centred")
                squares[piece] = squared.tile([P, CB, last - first], F32 if piece in whole[:2] else BF16, name="squares")
            z_ps = acc.tile([P, T], F32, name="z_ps", tag="acc")
            y = y_bf[b][:].rearrange("p h half position -> p h (half position)")
            for cb in range(CB):
                nc.tensor.matmul(
                    z_ps[:, : last - first],
                    wo_sb[:, cb, mb * P : (mb + 1) * P],
                    y[:, cb, first:last],
                    start=cb == 0,
                    stop=cb == CB - 1,
                )
            nc.vector.scalar_tensor_tensor(
                centred[piece][:, mb, :],
                z_ps[:, : last - first],
                vectors[:, mb, BO : BO + 1],
                x[mb][:, columns(piece)],
                ALU.add,
                ALU.add,
            )
            nc.scalar.square(squares[piece][:, mb, :], centred[piece][:, mb, :])

        def deviation(piece, pool, tag):
            b, first, last = piece
            blocks = [square_sum[piece][:]] if piece in square_sum else [squares[piece][:, i, :] for i in range(CB)]
            var_ps = pool.tile([P, T], F32, name="var_ps", tag=tag)
            for i, block in enumerate(blocks):
                nc.tensor.matmul(var_ps[:, : last - first], averager[:], block, start=i == 0, stop=i == len(blocks) - 1)
            inv_std[piece] = (tail if b < B - 1 else ending).tile([P, last - first], F32, name="inv_std")
            nc.scalar.activation(inv_std[piece][:], var_ps[:, : last - first], FUNC.Abs_reciprocal_sqrt, bias=eps[:])

        def normalise_block(piece, mb):
            b, first, last = piece
            normed = leaving.tile([P, last - first], F32, name="normed")
            result = stored.tile([P, last - first], F32, name="result")
            weight, bias = vectors[:, mb, LN_W : LN_W + 1], vectors[:, mb, LN_B : LN_B + 1]
            nc.vector.tensor_tensor(normed[:], centred[piece][:, mb, :], inv_std[piece][:], ALU.mult)
            if b == B - 1:
                nc.vector.tensor_scalar(result[:], normed[:], weight, bias, ALU.mult, ALU.add)
            else:
                nc.scalar.activation(result[:], normed[:], FUNC.Identity, bias=bias, scale=weight)
            nc.sync.dma_start(out[mb * P : (mb + 1) * P, columns(piece)], result[:])

        P_LEAD = 2
        STEPS = B * H
        Z_STEPS = (H + 4, 2 * H + 4, STEPS + 3)
        N_STEP = Z_STEPS[0] + 5
        all_queries, halves = (0, T), ((0, T // 2), (T // 2, T))
        items = [(b, h, all_queries, (pair,), pair) for b in range(B - 1) for h in range(H) for pair in range(2)]
        items += [(B - 1, h, halves[pair], tuple(range(pair + 1)), pair) for pair in range(2) for h in range(H)]
        half_0, half_1 = (B - 1, 0, T // 2), (B - 1, T // 2, T)
        for h in range(P_LEAD):
            project_k(0, h)
        for ib in range(P_LEAD):
            project_v(0, ib)
        for step in range(STEPS + 5):
            pb, ph = divmod(step + P_LEAD, H)
            scored, weighed, turned = (items[2 * s : 2 * s + 2] if 0 <= s < STEPS else [] for s in (step, step - 4, step - 5))
            if ph == 0 and 1 <= pb < B:
                new_caption(pb)
            if scored:
                scores(*scored[0][:4])
            if 1 <= pb < B:
                project_q(pb, ph)
            if turned:
                turn_back([(b, h, pair) for b, h, queries, key_pairs, pair in turned])
            if pb < B:
                project_k(pb, ph)
            if scored:
                scores(*scored[1][:4])
            if step == N_STEP:
                deviation(whole[0], acc, "acc")
            if step == STEPS:
                deviation(whole[1], score, "s_ps")
            if weighed:
                weigh(*weighed[0][:3], weighed[0][4])
            if pb < B:
                project_v(pb, ph)
            if weighed:
                weigh(*weighed[1][:3], weighed[1][4])
            if step == Z_STEPS[0] - 1:
                centre_wo()
            cx, later = divmod(step - 2, 2)
            if 0 <= cx < B:
                if later:
                    centre_x(cx)
                else:
                    x_sum[cx] = add_blocks([x[cb][:, cx * T : (cx + 1) * T] for cb in range(CB)])
            for piece, z_step in zip(whole, Z_STEPS):
                if step == z_step:
                    output_block(piece, 0)
                    output_block(piece, 1)
                if step == z_step + 1:
                    output_block(piece, 2)
                    output_block(piece, 3)
                    if piece in whole[:2]:
                        square_sum[piece] = add_blocks([squares[piece][:, i, :] for i in range(CB)])
            if N_STEP <= step < N_STEP + CB:
                normalise_block(whole[0], step - N_STEP)

        deviation(whole[2], score, "s_ps")
        for mb in range(CB):
            output_block(half_0, mb)
        deviation(half_0, score, "s_ps")
        for mb in range(CB):
            output_block(half_1, mb)
        deviation(half_1, acc, "acc")
        for mb in range(CB):
            normalise_block(whole[1], mb)
        for mb in range(CB):
            normalise_block(whole[2], mb)
        for mb in range(CB):
            normalise_block(half_0, mb)
        for mb in range(CB):
            normalise_block(half_1, mb)
